import numpy as np
import ml_dtypes


def mxq(x, axis, fmt="e4m3"):
    dtype, down = {"e4m3": (ml_dtypes.float8_e4m3fn, 7), "e5m2": (ml_dtypes.float8_e5m2, 14)}[fmt]
    v = np.moveaxis(np.asarray(x, np.float32).astype(ml_dtypes.bfloat16).astype(np.float64), axis, -1)
    blocks = v.reshape(v.shape[:-1] + (-1, 32))
    amax = np.abs(blocks).max(-1, keepdims=True)
    byte = np.maximum(np.where(amax > 0, np.frexp(amax)[1] - 1 + 127, 0) - down, 1)
    scale = np.exp2(byte - 127.0)
    codes = (blocks / scale).astype(np.float32).astype(dtype).astype(np.float64)
    return np.moveaxis((codes * scale).reshape(v.shape), -1, axis)


WIDE = False


def mx_kscale(k):
    if not WIDE:
        return np.ones(k)
    levels = np.array([10, -10, 5, -5, 0])
    if k % 512:
        return np.exp2(np.random.permutation(np.resize(levels, k // 32))).repeat(32)
    a = np.empty((k // 512, 16))
    for p in range(k // 512):
        a[p, :8] = np.random.permutation(np.resize(levels, 8))
        for g in range(8):
            far = levels[np.abs(levels - a[p, g]) >= 10]
            a[p, g + 8] = far[np.random.randint(len(far))]
    return np.exp2(a.ravel()).repeat(32)


BF16 = ml_dtypes.bfloat16


def bf(x):
    return np.asarray(x, np.float32).astype(BF16)


def f64(x):
    return np.asarray(x).astype(np.float64)


B, L, D, H, DH = 4, 2048, 512, 2, 64
THETA = 100000.0
E = H * DH


def rope(t):
    pos = np.arange(L, dtype=np.float64)
    inv_freq = 1.0 / THETA ** (np.arange(0, DH, 2, dtype=np.float64) / DH)
    ang = pos[:, None] * inv_freq[None, :]
    cos = np.cos(ang)[:, :, None]
    sin = np.sin(ang)[:, :, None]
    tp = t.reshape(*t.shape[:-1], DH // 2, 2)
    x1, x2 = tp[..., 0], tp[..., 1]
    rot = np.stack([-x2, x1], axis=-1)
    out = tp * cos + rot * sin
    return out.reshape(*t.shape)


def setup_inputs():
    s = mx_kscale(D)
    return {"x": bf(np.random.standard_normal((B, L, D)) * s),
            "W": bf(np.random.standard_normal((3 * E, D)) / np.sqrt(D) / s)}


def reference(x, W):
    qkv = mxq(f64(x), 2, "e4m3") @ mxq(f64(W), 1, "e4m3").T
    qkv = qkv.reshape(B, L, 3, H, DH)
    qkv = np.transpose(qkv, (0, 3, 1, 2, 4))
    q, k, v = qkv[..., 0, :], qkv[..., 1, :], qkv[..., 2, :]
    return rope(q), rope(k), np.ascontiguousarray(v)

@@ -1,0 +1,228 @@
+import math
+from contextlib import ExitStack
+
+import concourse.mybir as mybir
+from concourse.masks import make_identity
+
+F32 = mybir.dt.float32
+BF16 = mybir.dt.bfloat16
+I32 = mybir.dt.int32
+U32 = mybir.dt.uint32
+U8 = mybir.dt.uint8
+FP8X4 = mybir.dt.float8_e4m3fn_x4
+ALU = mybir.AluOpType
+ACT = mybir.ActivationFunctionType
+
+B, L, D, H, DH = 4, 2048, 512, 2, 64
+THETA = 100000.0
+P = 128
+PACK = 4
+PAIRS = DH // 2
+GROUPS = 2 * H
+TILES = L // P
+ROUND = 4
+ROUNDS = B * TILES // ROUND
+STORE_TILES = 2 * ROUND
+QK_COLS = 4 * P
+W_COLS = QK_COLS + P
+BLOCK_PARITY = (0, 1, 1, 0)
+
+FLOPS = 2 * B * L * D * 3 * H * DH
+
+
+def reduce_rotation_angles(nc, consts):
+    position = consts.tile([P, TILES], F32)
+    nc.gpsimd.iota(
+        position[:],
+        pattern=[[1, TILES]],
+        base=0,
+        channel_multiplier=TILES,
+        allow_small_or_imprecise_dtypes=True,
+    )
+    turns = consts.tile([P, PAIRS, TILES], F32)
+    for i in range(PAIRS):
+        nc.vector.tensor_scalar(
+            out=turns[:, i, :],
+            in0=position[:],
+            scalar1=THETA ** (-2.0 * i / DH) / (2.0 * math.pi),
+            scalar2=None,
+            op0=ALU.mult,
+        )
+    whole = consts.tile([P, PAIRS, TILES], I32)
+    nc.vector.tensor_copy(out=whole[:], in_=turns[:])
+    frac = consts.tile([P, PAIRS, TILES], F32)
+    nc.vector.tensor_tensor(out=frac[:], in0=turns[:], in1=whole[:], op=ALU.subtract)
+    minus_frac = consts.tile([P, PAIRS, TILES], F32)
+    nc.vector.scalar_tensor_tensor(
+        out=minus_frac[:], in0=frac[:], scalar=0.5, in1=frac[:], op0=ALU.is_gt, op1=ALU.subtract
+    )
+    quarter_minus_abs = consts.tile([P, PAIRS, TILES], F32)
+    nc.vector.scalar_tensor_tensor(
+        out=quarter_minus_abs[:],
+        in0=minus_frac[:],
+        scalar=-1.0,
+        in1=minus_frac[:],
+        op0=ALU.mult,
+        op1=ALU.min,
+    )
+    nc.vector.tensor_scalar_add(out=quarter_minus_abs[:], in0=quarter_minus_abs[:], scalar1=0.25)
+
+    return quarter_minus_abs[:].rearrange("p i t -> p t i"), minus_frac[:].rearrange("p i t -> p t i")
+
+
+def fill_rotation_table(nc, consts, cos_turns, sin_turns):
+    table = consts.tile([P, TILES, 4, PAIRS], F32)
+    nc.scalar.activation(out=table[:, :, 0, :], in_=cos_turns, func=ACT.Sin, scale=2.0 * math.pi)
+    nc.scalar.activation(out=table[:, :, 1, :], in_=cos_turns, func=ACT.Sin, scale=2.0 * math.pi)
+    nc.scalar.activation(out=table[:, :, 2, :], in_=sin_turns, func=ACT.Sin, scale=2.0 * math.pi)
+    nc.scalar.activation(out=table[:, :, 3, :], in_=sin_turns, func=ACT.Sin, scale=-2.0 * math.pi)
+    return table
+
+
+def transpose_words(nc, out, rows, identity):
+    words = rows.bitcast(F32)
+    for u in range(2):
+        nc.tensor.transpose(out[:, u, :], words[:, u : 2 * P : 2], identity[:])
+
+
+def quantise_weights(nc, consts, psum_v, w_rows, identity):
+    qk_t = psum_v.tile([P, 2, 2, P], F32, name="v_ps")
+    for chunk in range(2):
+        transpose_words(nc, qk_t[:, chunk], w_rows[:, chunk, :], identity)
+    v_t = psum_v.tile([P, 2, 2, P], F32, name="v_ps")
+    transpose_words(nc, v_t[:, 0], w_rows[:, 2, :], identity)
+
+    w_grouped = consts.tile([P, W_COLS * PACK], BF16, align_bytes=64)
+    w_words = w_grouped[:].bitcast(F32).rearrange("p (c u) -> p c u", u=2)
+    by_parity = qk_t[:].rearrange("p c u (m h) -> p h c m u", h=2)
+    for block, parity in enumerate(BLOCK_PARITY):
+        nc.vector.tensor_copy(
+            out=w_words[:, block * P : (block + 1) * P, :].rearrange("p (c m) u -> p c m u", c=2),
+            in_=by_parity[:, parity],
+        )
+    nc.vector.tensor_copy(out=w_words[:, QK_COLS:W_COLS, :], in_=v_t[:, 0].rearrange("p u r -> p r u"))
+
+    w_codes = consts.tile([P, W_COLS], U32, align_bytes=64)
+    w_scales = consts.tile([P, W_COLS], U8, align_bytes=64)
+    for lo, hi in ((0, QK_COLS), (QK_COLS, W_COLS)):
+        nc.vector.quantize_mx(
+            out=w_codes[:, lo:hi].bitcast(FP8X4),
+            scales=w_scales[:, lo:hi],
+            in_=w_grouped[:, lo * PACK : hi * PACK],
+        )
+    return w_codes, w_scales
+
+
+def tile_multiheadselfattention_pa_t_kernel(tc, x, W, out_0, out_1, out_2):
+    nc = tc.nc
+    with ExitStack() as ctx:
+        consts = ctx.enter_context(tc.tile_pool(name="consts", bufs=1))
+        x_pool = ctx.enter_context(tc.tile_pool(name="x_pool", bufs=ROUNDS))
+        stage = ctx.enter_context(tc.tile_pool(name="stage", bufs=2))
+        results = ctx.enter_context(tc.tile_pool(name="results", bufs=3))
+        psum_xt = ctx.enter_context(tc.psum_pool(name="psum_xt", bufs=2))
+        psum_qk = ctx.enter_context(tc.psum_pool(name="psum_qk", bufs=ROUND))
+        psum_v = ctx.enter_context(tc.psum_pool(name="psum_v", bufs=2))
+        ctx.enter_context(tc.manual_schedule())
+
+        w_rows = consts.tile([P, 3, D], BF16)
+        nc.scalar.dma_start(out=w_rows[:], in_=W.rearrange("(c p) k -> p c k", p=P))
+        x_rows = []
+        for r in range(ROUNDS):
+            b, first = divmod(r * ROUND, TILES)
+            x_tile = x_pool.tile([P, ROUND, D], BF16, name="x_tile")
+            nc.sync.dma_start(
+                out=x_tile[:],
+                in_=x[b].rearrange("(p t) c -> p t c", t=TILES)[:, first : first + ROUND, :],
+            )
+            x_rows.append(x_tile)
+
+        warm = consts.tile([P, 2], F32)
+        nc.vector.memset(warm[:], 0.0)
+        nc.scalar.activation(out=warm[:, 1:2], in_=warm[:, 0:1], func=ACT.Sin)
+
+        cos_turns, sin_turns = reduce_rotation_angles(nc, consts)
+        identity = consts.tile([P, P], F32)
+        make_identity(nc, identity[:])
+        w_codes, w_scales = quantise_weights(nc, consts, psum_v, w_rows, identity)
+
+        def transpose_round(r):
+            grouped = stage.tile([P, ROUND * P * PACK], BF16, align_bytes=64, name="grouped")
+            grouped_words = grouped[:].bitcast(F32).rearrange("p (j r u) -> p j r u", j=ROUND, u=2)
+            for pair in range(ROUND // 2):
+                xt = psum_xt.tile([P, 2, 2, P], F32, name="xt")
+                for j in range(2):
+                    transpose_words(nc, xt[:, j], x_rows[r][:, 2 * pair + j, :], identity)
+                nc.scalar.copy(
+                    out=grouped_words[:, 2 * pair : 2 * pair + 2],
+                    in_=xt[:].rearrange("p j u r -> p j r u"),
+                )
+            return grouped
+
+        def quantise_round(grouped):
+            x_codes = stage.tile([P, ROUND * P], U32, align_bytes=64, name="x_codes")
+            x_scales = stage.tile([P, ROUND * P], U8, align_bytes=64, name="x_scales")
+            nc.vector.quantize_mx(out=x_codes[:].bitcast(FP8X4), scales=x_scales[:], in_=grouped[:])
+            return x_codes, x_scales
+
+        def store(out, b, first, result):
+            rows = out[b].rearrange("h (p t) d -> p h t d", t=TILES)
+            nc.sync.dma_start(out=rows[:, :, first : first + STORE_TILES, :], in_=result)
+
+        grouped = transpose_round(0)
+        table = fill_rotation_table(nc, consts, cos_turns, sin_turns)
+        quantised = quantise_round(grouped)
+        for r in range(ROUNDS):
+            x_codes, x_scales = quantised
+            b, first = divmod(r * ROUND, TILES)
+            slot = first % STORE_TILES
+            if slot == 0:
+                qk_out = results.tile([P, GROUPS, STORE_TILES, DH], F32, name="qk_out")
+                v_out = results.tile([P, H, STORE_TILES, DH], F32, name="v_out")
+
+            if r + 1 < ROUNDS:
+                grouped = transpose_round(r + 1)
+
+            qk_banks = []
+            v_ps = psum_v.tile([P, ROUND, P], F32, name="v_ps")
+            for j in range(ROUND):
+                tokens = slice(j * P, (j + 1) * P)
+                qk_ps = psum_qk.tile([P, QK_COLS], F32, name="qk_ps")
+                for cols, acc in ((slice(0, QK_COLS), qk_ps[:]), (slice(QK_COLS, W_COLS), v_ps[:, j, :])):
+                    nc.tensor.matmul_mx(
+                        out=acc,
+                        lhsT=x_codes[:, tokens].bitcast(FP8X4),
+                        lhsT_scale=x_scales[:, tokens],
+                        rhs=w_codes[:, cols].bitcast(FP8X4),
+                        rhs_scale=w_scales[:, cols],
+                        start=True,
+                        stop=True,
+                    )
+                qk_banks.append(qk_ps)
+
+            if r + 1 < ROUNDS:
+                quantised = quantise_round(grouped)
+
+            products = results.tile([P, ROUND, QK_COLS], F32, name="products")
+            for j in range(ROUND):
+                nc.vector.tensor_tensor(
+                    out=products[:, j, :].rearrange("p (w g i) -> p w g i", w=4, g=GROUPS),
+                    in0=qk_banks[j][:].rearrange("p (w g i) -> p w g i", w=4, g=GROUPS),
+                    in1=table[:, first + j].unsqueeze(2).to_broadcast([P, 4, GROUPS, PAIRS]),
+                    op=ALU.mult,
+                )
+            nc.scalar.copy(
+                out=v_out[:, :, slot : slot + ROUND, :].rearrange("p h j d -> p j h d"),
+                in_=v_ps[:].rearrange("p j (h d) -> p j h d", h=H),
+            )
+            nc.gpsimd.tensor_tensor(
+                out=qk_out[:, :, slot : slot + ROUND, :].rearrange("p g j (i h) -> p j g i h", h=2),
+                in0=products[:, :, 0 : 2 * P].rearrange("p j (h g i) -> p j g i h", h=2, g=GROUPS),
+                in1=products[:, :, 2 * P : 4 * P].rearrange("p j (h g i) -> p j g i h", h=2, g=GROUPS),
+                op=ALU.add,
+            )
+
+            if slot + ROUND == STORE_TILES:
+                store(out_2, b, first - slot, v_out[:])
+                store(out_0, b, first - slot, qk_out[:, 0:H])
+                store(out_1, b, first - slot, qk_out[:, H:GROUPS])

@@ -23,14 +23,14 @@ TILES = L // P
 ROUND = 4
 ROUNDS = B * TILES // ROUND
 STORE_TILES = 2 * ROUND
-QK_COLS = 4 * P
+ROTATED = GROUPS * DH
+QK_COLS = 2 * ROTATED
 W_COLS = QK_COLS + P
-BLOCK_PARITY = (0, 1, 1, 0)
 
 FLOPS = 2 * B * L * D * 3 * H * DH
 
 
-def reduce_rotation_angles(nc, consts):
+def rotation_turns(nc, consts):
     position = consts.tile([P, TILES], F32)
     nc.gpsimd.iota(
         position[:],
@@ -39,24 +39,33 @@ def reduce_rotation_angles(nc, consts):
         channel_multiplier=TILES,
         allow_small_or_imprecise_dtypes=True,
     )
-    turns = consts.tile([P, PAIRS, TILES], F32)
-    for i in range(PAIRS):
+    turns = consts.tile([P, TILES, PAIRS], F32)
+    nc.vector.tensor_scalar(
+        out=turns[:, :, 0:1],
+        in0=position[:].unsqueeze(2),
+        scalar1=1.0 / (2.0 * math.pi),
+        scalar2=None,
+        op0=ALU.mult,
+    )
+    known = 1
+    while known < PAIRS:
         nc.vector.tensor_scalar(
-            out=turns[:, i, :],
-            in0=position[:],
-            scalar1=THETA ** (-2.0 * i / DH) / (2.0 * math.pi),
+            out=turns[:, :, known : 2 * known],
+            in0=turns[:, :, 0:known],
+            scalar1=THETA ** (-2.0 * known / DH),
             scalar2=None,
             op0=ALU.mult,
         )
-    whole = consts.tile([P, PAIRS, TILES], I32)
+        known *= 2
+    whole = consts.tile([P, TILES, PAIRS], I32)
     nc.vector.tensor_copy(out=whole[:], in_=turns[:])
-    frac = consts.tile([P, PAIRS, TILES], F32)
+    frac = consts.tile([P, TILES, PAIRS], F32)
     nc.vector.tensor_tensor(out=frac[:], in0=turns[:], in1=whole[:], op=ALU.subtract)
-    minus_frac = consts.tile([P, PAIRS, TILES], F32)
+    minus_frac = consts.tile([P, TILES, PAIRS], F32)
     nc.vector.scalar_tensor_tensor(
         out=minus_frac[:], in0=frac[:], scalar=0.5, in1=frac[:], op0=ALU.is_gt, op1=ALU.subtract
     )
-    quarter_minus_abs = consts.tile([P, PAIRS, TILES], F32)
+    quarter_minus_abs = consts.tile([P, TILES, PAIRS], F32)
     nc.vector.scalar_tensor_tensor(
         out=quarter_minus_abs[:],
         in0=minus_frac[:],
@@ -66,16 +75,29 @@ def reduce_rotation_angles(nc, consts):
         op1=ALU.min,
     )
     nc.vector.tensor_scalar_add(out=quarter_minus_abs[:], in0=quarter_minus_abs[:], scalar1=0.25)
+    return quarter_minus_abs, minus_frac
 
-    return quarter_minus_abs[:].rearrange("p i t -> p t i"), minus_frac[:].rearrange("p i t -> p t i")
 
-
-def fill_rotation_table(nc, consts, cos_turns, sin_turns):
-    table = consts.tile([P, TILES, 4, PAIRS], F32)
-    nc.scalar.activation(out=table[:, :, 0, :], in_=cos_turns, func=ACT.Sin, scale=2.0 * math.pi)
-    nc.scalar.activation(out=table[:, :, 1, :], in_=cos_turns, func=ACT.Sin, scale=2.0 * math.pi)
-    nc.scalar.activation(out=table[:, :, 2, :], in_=sin_turns, func=ACT.Sin, scale=2.0 * math.pi)
-    nc.scalar.activation(out=table[:, :, 3, :], in_=sin_turns, func=ACT.Sin, scale=-2.0 * math.pi)
+def fill_rotation_table(nc, consts, cos_turns, minus_turns):
+    signs = consts.tile([P, 2], F32)
+    nc.gpsimd.memset(signs[:, 0:1], 1.0)
+    nc.gpsimd.memset(signs[:, 1:2], -1.0)
+    pair_shape = [P, TILES, PAIRS, 2]
+    signed_turns = consts.tile(pair_shape, F32)
+    nc.gpsimd.tensor_tensor(
+        out=signed_turns[:].rearrange("p t i h -> p (t i) h"),
+        in0=minus_turns[:].rearrange("p t i -> p (t i)").unsqueeze(2).to_broadcast([P, TILES * PAIRS, 2]),
+        in1=signs[:].unsqueeze(1).to_broadcast([P, TILES * PAIRS, 2]),
+        op=ALU.mult,
+    )
+    table = consts.tile([P, TILES, 2, PAIRS, 2], F32)
+    nc.scalar.activation(
+        out=table[:, :, 0],
+        in_=cos_turns[:].unsqueeze(3).to_broadcast(pair_shape),
+        func=ACT.Sin,
+        scale=2.0 * math.pi,
+    )
+    nc.scalar.activation(out=table[:, :, 1], in_=signed_turns[:], func=ACT.Sin, scale=2.0 * math.pi)
     return table
 
 
@@ -94,12 +116,14 @@ def quantise_weights(nc, consts, psum_v, w_rows, identity):
 
     w_grouped = consts.tile([P, W_COLS * PACK], BF16, align_bytes=64)
     w_words = w_grouped[:].bitcast(F32).rearrange("p (c u) -> p c u", u=2)
+    nc.vector.tensor_copy(
+        out=w_words[:, 0:ROTATED, :].rearrange("p (c r) u -> p c r u", c=2),
+        in_=qk_t[:].rearrange("p c u r -> p c r u"),
+    )
+    swapped = w_words[:, ROTATED:QK_COLS, :].rearrange("p (c m h) u -> p h c m u", c=2, h=2)
     by_parity = qk_t[:].rearrange("p c u (m h) -> p h c m u", h=2)
-    for block, parity in enumerate(BLOCK_PARITY):
-        nc.vector.tensor_copy(
-            out=w_words[:, block * P : (block + 1) * P, :].rearrange("p (c m) u -> p c m u", c=2),
-            in_=by_parity[:, parity],
-        )
+    for parity in range(2):
+        nc.vector.tensor_copy(out=swapped[:, parity], in_=by_parity[:, 1 - parity])
     nc.vector.tensor_copy(out=w_words[:, QK_COLS:W_COLS, :], in_=v_t[:, 0].rearrange("p u r -> p r u"))
 
     w_codes = consts.tile([P, W_COLS], U32, align_bytes=64)
@@ -141,7 +165,7 @@ def tile_multiheadselfattention_pa_t_kernel(tc, x, W, out_0, out_1, out_2):
         nc.vector.memset(warm[:], 0.0)
         nc.scalar.activation(out=warm[:, 1:2], in_=warm[:, 0:1], func=ACT.Sin)
 
-        cos_turns, sin_turns = reduce_rotation_angles(nc, consts)
+        cos_turns, minus_turns = rotation_turns(nc, consts)
         identity = consts.tile([P, P], F32)
         make_identity(nc, identity[:])
         w_codes, w_scales = quantise_weights(nc, consts, psum_v, w_rows, identity)
@@ -170,7 +194,7 @@ def tile_multiheadselfattention_pa_t_kernel(tc, x, W, out_0, out_1, out_2):
             nc.sync.dma_start(out=rows[:, :, first : first + STORE_TILES, :], in_=result)
 
         grouped = transpose_round(0)
-        table = fill_rotation_table(nc, consts, cos_turns, sin_turns)
+        table = fill_rotation_table(nc, consts, cos_turns, minus_turns)
         quantised = quantise_round(grouped)
         for r in range(ROUNDS):
             x_codes, x_scales = quantised
@@ -206,9 +230,12 @@ def tile_multiheadselfattention_pa_t_kernel(tc, x, W, out_0, out_1, out_2):
             products = results.tile([P, ROUND, QK_COLS], F32, name="products")
             for j in range(ROUND):
                 nc.vector.tensor_tensor(
-                    out=products[:, j, :].rearrange("p (w g i) -> p w g i", w=4, g=GROUPS),
-                    in0=qk_banks[j][:].rearrange("p (w g i) -> p w g i", w=4, g=GROUPS),
-                    in1=table[:, first + j].unsqueeze(2).to_broadcast([P, 4, GROUPS, PAIRS]),
+                    out=products[:, j, :].rearrange("p (w g d) -> p w g d", w=2, g=GROUPS),
+                    in0=qk_banks[j][:].rearrange("p (w g d) -> p w g d", w=2, g=GROUPS),
+                    in1=table[:, first + j]
+                    .rearrange("p w i h -> p w (i h)")
+                    .unsqueeze(2)
+                    .to_broadcast([P, 2, GROUPS, DH]),
                     op=ALU.mult,
                 )
             nc.scalar.copy(
@@ -216,9 +243,9 @@ def tile_multiheadselfattention_pa_t_kernel(tc, x, W, out_0, out_1, out_2):
                 in_=v_ps[:].rearrange("p j (h d) -> p j h d", h=H),
             )
             nc.gpsimd.tensor_tensor(
-                out=qk_out[:, :, slot : slot + ROUND, :].rearrange("p g j (i h) -> p j g i h", h=2),
-                in0=products[:, :, 0 : 2 * P].rearrange("p j (h g i) -> p j g i h", h=2, g=GROUPS),
-                in1=products[:, :, 2 * P : 4 * P].rearrange("p j (h g i) -> p j g i h", h=2, g=GROUPS),
+                out=qk_out[:, :, slot : slot + ROUND, :].rearrange("p g j d -> p j g d"),
+                in0=products[:, :, 0:ROTATED].rearrange("p j (g d) -> p j g d", g=GROUPS),
+                in1=products[:, :, ROTATED:QK_COLS].rearrange("p j (g d) -> p j g d", g=GROUPS),
                 op=ALU.add,
             )
 

@@ -19,35 +19,48 @@ P = 128
 PACK = 4
 PAIRS = DH // 2
 GROUPS = 2 * H
-TILES = L // P
-ROUND = 4
-ROUNDS = B * TILES // ROUND
-STORE_TILES = 2 * ROUND
 ROTATED = GROUPS * DH
-QK_COLS = 2 * ROTATED
-W_COLS = QK_COLS + P
+VALUES = H * DH
+W_COLS = VALUES + ROTATED
+TILES = L // P
+PAIR = 2
+MAX_ROUND = 4
+MAX_STORE = 8
+DIRECT = 8
+AHEAD = 2
 
 FLOPS = 2 * B * L * D * 3 * H * DH
 
 
-def rotation_turns(nc, consts):
-    position = consts.tile([P, TILES], F32)
-    nc.gpsimd.iota(
-        position[:],
-        pattern=[[1, TILES]],
-        base=0,
-        channel_multiplier=TILES,
-        allow_small_or_imprecise_dtypes=True,
-    )
+def plan():
+    rounds, stores = [], []
+    for b in range(B):
+        sizes = [MAX_ROUND] * (TILES // MAX_ROUND)
+        store_sizes = [MAX_STORE] * (TILES // MAX_STORE)
+        if b == 0:
+            sizes = [PAIR, PAIR] + sizes[1:]
+        if b == B - 1:
+            sizes = sizes[:-1] + [PAIR, PAIR]
+            store_sizes = store_sizes[:-1] + [MAX_ROUND, PAIR, PAIR]
+        for lengths, out in ((sizes, rounds), (store_sizes, stores)):
+            first = 0
+            for n in lengths:
+                out.append((b, first, n))
+                first += n
+    return rounds, stores
+
+
+def rotation_turns(nc, consts, position):
     turns = consts.tile([P, TILES, PAIRS], F32)
-    nc.vector.tensor_scalar(
-        out=turns[:, :, 0:1],
-        in0=position[:].unsqueeze(2),
-        scalar1=1.0 / (2.0 * math.pi),
-        scalar2=None,
-        op0=ALU.mult,
-    )
-    known = 1
+    for i in range(DIRECT):
+        nc.vector.tensor_scalar(
+            out=turns[:, :, i : i + 1],
+            in0=position[:].unsqueeze(2),
+            scalar1=THETA ** (-2.0 * i / DH) / (2.0 * math.pi),
+            scalar2=None,
+            op0=ALU.mult,
+        )
+    known = DIRECT
     while known < PAIRS:
         nc.vector.tensor_scalar(
             out=turns[:, :, known : 2 * known],
@@ -65,40 +78,25 @@ def rotation_turns(nc, consts):
     nc.vector.scalar_tensor_tensor(
         out=minus_frac[:], in0=frac[:], scalar=0.5, in1=frac[:], op0=ALU.is_gt, op1=ALU.subtract
     )
-    quarter_minus_abs = consts.tile([P, TILES, PAIRS], F32)
+    minus_abs = consts.tile([P, TILES, PAIRS], F32)
     nc.vector.scalar_tensor_tensor(
-        out=quarter_minus_abs[:],
-        in0=minus_frac[:],
-        scalar=-1.0,
-        in1=minus_frac[:],
-        op0=ALU.mult,
-        op1=ALU.min,
+        out=minus_abs[:], in0=minus_frac[:], scalar=-1.0, in1=minus_frac[:], op0=ALU.mult, op1=ALU.min
     )
-    nc.vector.tensor_scalar_add(out=quarter_minus_abs[:], in0=quarter_minus_abs[:], scalar1=0.25)
-    return quarter_minus_abs, minus_frac
+    return minus_abs, minus_frac
 
 
-def fill_rotation_table(nc, consts, cos_turns, minus_turns):
-    signs = consts.tile([P, 2], F32)
-    nc.gpsimd.memset(signs[:, 0:1], 1.0)
-    nc.gpsimd.memset(signs[:, 1:2], -1.0)
-    pair_shape = [P, TILES, PAIRS, 2]
-    signed_turns = consts.tile(pair_shape, F32)
-    nc.gpsimd.tensor_tensor(
-        out=signed_turns[:].rearrange("p t i h -> p (t i) h"),
-        in0=minus_turns[:].rearrange("p t i -> p (t i)").unsqueeze(2).to_broadcast([P, TILES * PAIRS, 2]),
-        in1=signs[:].unsqueeze(1).to_broadcast([P, TILES * PAIRS, 2]),
-        op=ALU.mult,
-    )
-    table = consts.tile([P, TILES, 2, PAIRS, 2], F32)
+def fill_rotation_table(nc, table, minus_abs, minus_frac, lo, hi):
     nc.scalar.activation(
-        out=table[:, :, 0],
-        in_=cos_turns[:].unsqueeze(3).to_broadcast(pair_shape),
+        out=table[:, lo:hi, 0],
+        in_=minus_abs[:, lo:hi].unsqueeze(3).to_broadcast([P, hi - lo, PAIRS, 2]),
         func=ACT.Sin,
         scale=2.0 * math.pi,
+        bias=0.5 * math.pi,
     )
-    nc.scalar.activation(out=table[:, :, 1], in_=signed_turns[:], func=ACT.Sin, scale=2.0 * math.pi)
-    return table
+    for h, sign in ((0, 1.0), (1, -1.0)):
+        nc.scalar.activation(
+            out=table[:, lo:hi, 1, :, h], in_=minus_frac[:, lo:hi], func=ACT.Sin, scale=sign * 2.0 * math.pi
+        )
 
 
 def transpose_words(nc, out, rows, identity):
@@ -107,57 +105,28 @@ def transpose_words(nc, out, rows, identity):
         nc.tensor.transpose(out[:, u, :], words[:, u : 2 * P : 2], identity[:])
 
 
-def quantise_weights(nc, consts, psum_v, w_rows, identity):
-    qk_t = psum_v.tile([P, 2, 2, P], F32, name="v_ps")
-    for chunk in range(2):
-        transpose_words(nc, qk_t[:, chunk], w_rows[:, chunk, :], identity)
-    v_t = psum_v.tile([P, 2, 2, P], F32, name="v_ps")
-    transpose_words(nc, v_t[:, 0], w_rows[:, 2, :], identity)
-
-    w_grouped = consts.tile([P, W_COLS * PACK], BF16, align_bytes=64)
-    w_words = w_grouped[:].bitcast(F32).rearrange("p (c u) -> p c u", u=2)
-    nc.vector.tensor_copy(
-        out=w_words[:, 0:ROTATED, :].rearrange("p (c r) u -> p c r u", c=2),
-        in_=qk_t[:].rearrange("p c u r -> p c r u"),
-    )
-    swapped = w_words[:, ROTATED:QK_COLS, :].rearrange("p (c m h) u -> p h c m u", c=2, h=2)
-    by_parity = qk_t[:].rearrange("p c u (m h) -> p h c m u", h=2)
-    for parity in range(2):
-        nc.vector.tensor_copy(out=swapped[:, parity], in_=by_parity[:, 1 - parity])
-    nc.vector.tensor_copy(out=w_words[:, QK_COLS:W_COLS, :], in_=v_t[:, 0].rearrange("p u r -> p r u"))
-
-    w_codes = consts.tile([P, W_COLS], U32, align_bytes=64)
-    w_scales = consts.tile([P, W_COLS], U8, align_bytes=64)
-    for lo, hi in ((0, QK_COLS), (QK_COLS, W_COLS)):
-        nc.vector.quantize_mx(
-            out=w_codes[:, lo:hi].bitcast(FP8X4),
-            scales=w_scales[:, lo:hi],
-            in_=w_grouped[:, lo * PACK : hi * PACK],
-        )
-    return w_codes, w_scales
-
-
 def tile_multiheadselfattention_pa_t_kernel(tc, x, W, out_0, out_1, out_2):
     nc = tc.nc
+    rounds, stores = plan()
     with ExitStack() as ctx:
         consts = ctx.enter_context(tc.tile_pool(name="consts", bufs=1))
-        x_pool = ctx.enter_context(tc.tile_pool(name="x_pool", bufs=ROUNDS))
-        stage = ctx.enter_context(tc.tile_pool(name="stage", bufs=2))
-        results = ctx.enter_context(tc.tile_pool(name="results", bufs=3))
+        x_pool = ctx.enter_context(tc.tile_pool(name="x_pool", bufs=len(rounds)))
+        stage = ctx.enter_context(tc.tile_pool(name="stage", bufs=4))
+        products_pool = ctx.enter_context(tc.tile_pool(name="products_pool", bufs=3))
+        results = ctx.enter_context(tc.tile_pool(name="results", bufs=4))
         psum_xt = ctx.enter_context(tc.psum_pool(name="psum_xt", bufs=2))
-        psum_qk = ctx.enter_context(tc.psum_pool(name="psum_qk", bufs=ROUND))
+        psum_qk = ctx.enter_context(tc.psum_pool(name="psum_qk", bufs=4))
         psum_v = ctx.enter_context(tc.psum_pool(name="psum_v", bufs=2))
         ctx.enter_context(tc.manual_schedule())
 
         w_rows = consts.tile([P, 3, D], BF16)
-        nc.scalar.dma_start(out=w_rows[:], in_=W.rearrange("(c p) k -> p c k", p=P))
+        nc.sync.dma_start(out=w_rows[:], in_=W.rearrange("(c p) k -> p c k", p=P))
         x_rows = []
-        for r in range(ROUNDS):
-            b, first = divmod(r * ROUND, TILES)
-            x_tile = x_pool.tile([P, ROUND, D], BF16, name="x_tile")
+        for b, first, n in rounds:
+            x_tile = x_pool.tile([P, MAX_ROUND, D], BF16, name="x_tile")
             nc.sync.dma_start(
-                out=x_tile[:],
-                in_=x[b].rearrange("(p t) c -> p t c", t=TILES)[:, first : first + ROUND, :],
+                out=x_tile[:, 0:n, :],
+                in_=x[b].rearrange("(p t) c -> p t c", t=TILES)[:, first : first + n, :],
             )
             x_rows.append(x_tile)
 
@@ -165,54 +134,57 @@ def tile_multiheadselfattention_pa_t_kernel(tc, x, W, out_0, out_1, out_2):
         nc.vector.memset(warm[:], 0.0)
         nc.scalar.activation(out=warm[:, 1:2], in_=warm[:, 0:1], func=ACT.Sin)
 
-        cos_turns, minus_turns = rotation_turns(nc, consts)
+        position = consts.tile([P, TILES], F32)
+        nc.gpsimd.iota(
+            position[:],
+            pattern=[[1, TILES]],
+            base=0,
+            channel_multiplier=TILES,
+            allow_small_or_imprecise_dtypes=True,
+        )
         identity = consts.tile([P, P], F32)
         make_identity(nc, identity[:])
-        w_codes, w_scales = quantise_weights(nc, consts, psum_v, w_rows, identity)
 
-        def transpose_round(r):
-            grouped = stage.tile([P, ROUND * P * PACK], BF16, align_bytes=64, name="grouped")
-            grouped_words = grouped[:].bitcast(F32).rearrange("p (j r u) -> p j r u", j=ROUND, u=2)
-            for pair in range(ROUND // 2):
-                xt = psum_xt.tile([P, 2, 2, P], F32, name="xt")
-                for j in range(2):
-                    transpose_words(nc, xt[:, j], x_rows[r][:, 2 * pair + j, :], identity)
-                nc.scalar.copy(
-                    out=grouped_words[:, 2 * pair : 2 * pair + 2],
-                    in_=xt[:].rearrange("p j u r -> p j r u"),
-                )
-            return grouped
+        table = consts.tile([P, TILES, 2, PAIRS, 2], F32)
+        minus_abs, minus_frac = rotation_turns(nc, consts, position)
 
-        def quantise_round(grouped):
-            x_codes = stage.tile([P, ROUND * P], U32, align_bytes=64, name="x_codes")
-            x_scales = stage.tile([P, ROUND * P], U8, align_bytes=64, name="x_scales")
-            nc.vector.quantize_mx(out=x_codes[:].bitcast(FP8X4), scales=x_scales[:], in_=grouped[:])
+        grouped_rounds = {}
+
+        def transpose_pair(r, k):
+            if k == 0:
+                grouped = stage.tile([P, MAX_ROUND * P * PACK], BF16, align_bytes=64, name="grouped")
+                grouped_rounds[r] = grouped
+            xt = psum_xt.tile([P, PAIR, 2, P], F32, name="xt")
+            for j in range(PAIR):
+                transpose_words(nc, xt[:, j], x_rows[r][:, PAIR * k + j, :], identity)
+            grouped_words = grouped_rounds[r][:].bitcast(F32).rearrange("p (j r u) -> p j r u", j=MAX_ROUND, u=2)
+            nc.scalar.copy(
+                out=grouped_words[:, PAIR * k : PAIR * k + PAIR],
+                in_=xt[:].rearrange("p j u r -> p j r u"),
+            )
+
+        def quantise_round(r):
+            n = rounds[r][2]
+            grouped = grouped_rounds.pop(r)
+            x_codes = stage.tile([P, MAX_ROUND * P], U32, align_bytes=64, name="x_codes")
+            x_scales = stage.tile([P, MAX_ROUND * P], U8, align_bytes=64, name="x_scales")
+            nc.vector.quantize_mx(
+                out=x_codes[:, 0 : n * P].bitcast(FP8X4),
+                scales=x_scales[:, 0 : n * P],
+                in_=grouped[:, 0 : n * P * PACK],
+            )
             return x_codes, x_scales
 
-        def store(out, b, first, result):
-            rows = out[b].rearrange("h (p t) d -> p h t d", t=TILES)
-            nc.sync.dma_start(out=rows[:, :, first : first + STORE_TILES, :], in_=result)
-
-        grouped = transpose_round(0)
-        table = fill_rotation_table(nc, consts, cos_turns, minus_turns)
-        quantised = quantise_round(grouped)
-        for r in range(ROUNDS):
+        def multiply_pair(k, quantised):
             x_codes, x_scales = quantised
-            b, first = divmod(r * ROUND, TILES)
-            slot = first % STORE_TILES
-            if slot == 0:
-                qk_out = results.tile([P, GROUPS, STORE_TILES, DH], F32, name="qk_out")
-                v_out = results.tile([P, H, STORE_TILES, DH], F32, name="v_out")
-
-            if r + 1 < ROUNDS:
-                grouped = transpose_round(r + 1)
-
-            qk_banks = []
-            v_ps = psum_v.tile([P, ROUND, P], F32, name="v_ps")
-            for j in range(ROUND):
-                tokens = slice(j * P, (j + 1) * P)
-                qk_ps = psum_qk.tile([P, QK_COLS], F32, name="qk_ps")
-                for cols, acc in ((slice(0, QK_COLS), qk_ps[:]), (slice(QK_COLS, W_COLS), v_ps[:, j, :])):
+            qk_ps = psum_qk.tile([P, PAIR, ROTATED], F32, name="qk_ps")
+            v_ps = psum_v.tile([P, PAIR, 2 * VALUES], F32, name="v_ps")
+            for j in range(PAIR):
+                tokens = slice((PAIR * k + j) * P, (PAIR * k + j + 1) * P)
+                for cols, acc in (
+                    (slice(VALUES, W_COLS), qk_ps[:, j, :]),
+                    (slice(0, 2 * VALUES), v_ps[:, j, :]),
+                ):
                     nc.tensor.matmul_mx(
                         out=acc,
                         lhsT=x_codes[:, tokens].bitcast(FP8X4),
@@ -222,34 +194,89 @@ def tile_multiheadselfattention_pa_t_kernel(tc, x, W, out_0, out_1, out_2):
                         start=True,
                         stop=True,
                     )
-                qk_banks.append(qk_ps)
+            return qk_ps, v_ps
 
-            if r + 1 < ROUNDS:
-                quantised = quantise_round(grouped)
+        w_codes = consts.tile([P, W_COLS], U32, align_bytes=64)
+        w_scales = consts.tile([P, W_COLS], U8, align_bytes=64)
+        w_grouped = consts.tile([P, W_COLS * PACK], BF16, align_bytes=64)
+        w_words = w_grouped[:].bitcast(F32).rearrange("p (c r u) -> p c r u", c=3, u=2)
+        qk_t = psum_v.tile([P, 2, 2, P], F32, name="v_ps")
+        for chunk in range(2):
+            transpose_words(nc, qk_t[:, chunk], w_rows[:, chunk, :], identity)
+        nc.vector.tensor_copy(out=w_words[:, 1:3], in_=qk_t[:].rearrange("p c u r -> p c r u"))
+        transpose_pair(0, 0)
+        v_t = psum_v.tile([P, 2, 2, P], F32, name="v_ps")
+        transpose_words(nc, v_t[:, 0], w_rows[:, 2, :], identity)
+        nc.vector.quantize_mx(
+            out=w_codes[:, VALUES:W_COLS].bitcast(FP8X4),
+            scales=w_scales[:, VALUES:W_COLS],
+            in_=w_grouped[:, VALUES * PACK : W_COLS * PACK],
+        )
+        quantised = quantise_round(0)
+        nc.scalar.copy(out=w_words[:, 0], in_=v_t[:, 0].rearrange("p u r -> p r u"))
+        filled = MAX_ROUND
+        fill_rotation_table(nc, table, minus_abs, minus_frac, 0, filled)
+        for k in range(rounds[1][2] // PAIR):
+            transpose_pair(1, k)
+        nc.vector.quantize_mx(
+            out=w_codes[:, 0:VALUES].bitcast(FP8X4),
+            scales=w_scales[:, 0:VALUES],
+            in_=w_grouped[:, 0 : VALUES * PACK],
+        )
 
-            products = results.tile([P, ROUND, QK_COLS], F32, name="products")
-            for j in range(ROUND):
-                nc.vector.tensor_tensor(
-                    out=products[:, j, :].rearrange("p (w g d) -> p w g d", w=2, g=GROUPS),
-                    in0=qk_banks[j][:].rearrange("p (w g d) -> p w g d", w=2, g=GROUPS),
-                    in1=table[:, first + j]
-                    .rearrange("p w i h -> p w (i h)")
-                    .unsqueeze(2)
-                    .to_broadcast([P, 2, GROUPS, DH]),
-                    op=ALU.mult,
-                )
-            nc.scalar.copy(
-                out=v_out[:, :, slot : slot + ROUND, :].rearrange("p h j d -> p j h d"),
-                in_=v_ps[:].rearrange("p j (h d) -> p j h d", h=H),
-            )
-            nc.gpsimd.tensor_tensor(
-                out=qk_out[:, :, slot : slot + ROUND, :].rearrange("p g j d -> p j g d"),
-                in0=products[:, :, 0:ROTATED].rearrange("p j (g d) -> p j g d", g=GROUPS),
-                in1=products[:, :, ROTATED:QK_COLS].rearrange("p j (g d) -> p j g d", g=GROUPS),
+        store_index = 0
+        for r, (b, first, n) in enumerate(rounds):
+            store_first, store_n = stores[store_index][1:]
+            slot = first - store_first
+            if slot == 0:
+                qk_out = results.tile([P, GROUPS, MAX_STORE, DH], F32, name="qk_out")
+                v_out = results.tile([P, H, MAX_STORE, DH], F32, name="v_out")
+
+            ahead_pairs = rounds[r + AHEAD][2] // PAIR if r + AHEAD < len(rounds) else 0
+            qk_banks = []
+            for k in range(max(ahead_pairs, n // PAIR)):
+                if k < ahead_pairs:
+                    transpose_pair(r + AHEAD, k)
+                if k < n // PAIR:
+                    qk_ps, v_ps = multiply_pair(k, quantised)
+                    qk_banks.append(qk_ps)
+                    lo = slot + PAIR * k
+                    nc.scalar.copy(
+                        out=v_out[:, :, lo : lo + PAIR, :].rearrange("p h j d -> p j h d"),
+                        in_=v_ps[:, :, 0:VALUES].rearrange("p j (h d) -> p j h d", h=H),
+                    )
+            if r + 1 < len(rounds):
+                quantised = quantise_round(r + 1)
+            if filled < TILES:
+                fill_rotation_table(nc, table, minus_abs, minus_frac, filled, filled + MAX_ROUND)
+                filled += MAX_ROUND
+
+            products = products_pool.tile([P, 2, MAX_ROUND, ROTATED], F32, name="products")
+            pair_shape = [P, PAIR, GROUPS, PAIRS, 2]
+            for k in range(n // PAIR):
+                t = first + PAIR * k
+                qk = qk_banks[k][:].rearrange("p j (g i h) -> p j g i h", g=GROUPS, h=2)
+                for term, operand in ((0, qk), (1, qk[:, :, :, :, ::-1])):
+                    nc.vector.tensor_tensor(
+                        out=products[:, term, PAIR * k : PAIR * k + PAIR, :].rearrange(
+                            "p j (g i h) -> p j g i h", g=GROUPS, h=2
+                        ),
+                        in0=operand,
+                        in1=table[:, t : t + PAIR, term].unsqueeze(2).to_broadcast(pair_shape),
+                        op=ALU.mult,
+                    )
+            adder = nc.vector if r + 1 == len(rounds) else nc.gpsimd
+            adder.tensor_tensor(
+                out=qk_out[:, :, slot : slot + n, :].rearrange("p g j d -> p j g d"),
+                in0=products[:, 0, 0:n, :].rearrange("p j (g d) -> p j g d", g=GROUPS),
+                in1=products[:, 1, 0:n, :].rearrange("p j (g d) -> p j g d", g=GROUPS),
                 op=ALU.add,
             )
 
-            if slot + ROUND == STORE_TILES:
-                store(out_2, b, first - slot, v_out[:])
-                store(out_0, b, first - slot, qk_out[:, 0:H])
-                store(out_1, b, first - slot, qk_out[:, H:GROUPS])
+            if slot + n == store_n:
+                for out, result in ((out_2, v_out[:]), (out_0, qk_out[:, 0:H]), (out_1, qk_out[:, H:GROUPS])):
+                    rows = out[b].rearrange("h (p t) d -> p h t d", t=TILES)
+                    nc.sync.dma_start(
+                        out=rows[:, :, store_first : store_first + store_n, :], in_=result[:, :, 0:store_n, :]
+                    )
+                store_index += 1

@@ -178,12 +178,12 @@ def tile_multiheadselfattention_pa_t_kernel(tc, x, W, out_0, out_1, out_2):
         def multiply_pair(k, quantised):
             x_codes, x_scales = quantised
             qk_ps = psum_qk.tile([P, PAIR, ROTATED], F32, name="qk_ps")
-            v_ps = psum_v.tile([P, PAIR, 2 * VALUES], F32, name="v_ps")
+            v_ps = psum_v.tile([P, PAIR, VALUES], F32, name="v_ps")
             for j in range(PAIR):
                 tokens = slice((PAIR * k + j) * P, (PAIR * k + j + 1) * P)
                 for cols, acc in (
                     (slice(VALUES, W_COLS), qk_ps[:, j, :]),
-                    (slice(0, 2 * VALUES), v_ps[:, j, :]),
+                    (slice(0, VALUES), v_ps[:, j, :]),
                 ):
                     nc.tensor.matmul_mx(
                         out=acc,
@@ -243,7 +243,7 @@ def tile_multiheadselfattention_pa_t_kernel(tc, x, W, out_0, out_1, out_2):
                     lo = slot + PAIR * k
                     nc.scalar.copy(
                         out=v_out[:, :, lo : lo + PAIR, :].rearrange("p h j d -> p j h d"),
-                        in_=v_ps[:, :, 0:VALUES].rearrange("p j (h d) -> p j h d", h=H),
+                        in_=v_ps[:].rearrange("p j (h d) -> p j h d", h=H),
                     )
             if r + 1 < len(rounds):
                 quantised = quantise_round(r + 1)

@@ -93,7 +93,7 @@ def fill_rotation_table(nc, table, minus_abs, minus_frac, lo, hi):
         scale=2.0 * math.pi,
         bias=0.5 * math.pi,
     )
-    for h, sign in ((0, 1.0), (1, -1.0)):
+    for h, sign in ((0, -1.0), (1, 1.0)):
         nc.scalar.activation(
             out=table[:, lo:hi, 1, :, h], in_=minus_frac[:, lo:hi], func=ACT.Sin, scale=sign * 2.0 * math.pi
         )
@@ -110,8 +110,7 @@ def tile_multiheadselfattention_pa_t_kernel(tc, x, W, out_0, out_1, out_2):
     rounds, stores = plan()
     with ExitStack() as ctx:
         consts = ctx.enter_context(tc.tile_pool(name="consts", bufs=1))
-        x_pool = ctx.enter_context(tc.tile_pool(name="x_pool", bufs=len(rounds)))
-        stage = ctx.enter_context(tc.tile_pool(name="stage", bufs=4))
+        stage = ctx.enter_context(tc.tile_pool(name="stage", bufs=5))
         products_pool = ctx.enter_context(tc.tile_pool(name="products_pool", bufs=3))
         results = ctx.enter_context(tc.tile_pool(name="results", bufs=4))
         psum_xt = ctx.enter_context(tc.psum_pool(name="psum_xt", bufs=2))
@@ -120,15 +119,22 @@ def tile_multiheadselfattention_pa_t_kernel(tc, x, W, out_0, out_1, out_2):
         ctx.enter_context(tc.manual_schedule())
 
         w_rows = consts.tile([P, 3, D], BF16)
-        nc.sync.dma_start(out=w_rows[:], in_=W.rearrange("(c p) k -> p c k", p=P))
         x_rows = []
-        for b, first, n in rounds:
-            x_tile = x_pool.tile([P, MAX_ROUND, D], BF16, name="x_tile")
+
+        def load_weights(chunk):
+            nc.sync.dma_start(out=w_rows[:, chunk, :], in_=W[chunk * P : (chunk + 1) * P, :])
+
+        load_weights(0)
+        load_weights(1)
+        for r, (b, first, n) in enumerate(rounds):
+            x_tile = consts.tile([P, n, D], BF16, name="x_tile%d" % r)
             nc.sync.dma_start(
-                out=x_tile[:, 0:n, :],
+                out=x_tile[:],
                 in_=x[b].rearrange("(p t) c -> p t c", t=TILES)[:, first : first + n, :],
             )
             x_rows.append(x_tile)
+            if r == 0:
+                load_weights(2)
 
         warm = consts.tile([P, 2], F32)
         nc.vector.memset(warm[:], 0.0)
@@ -173,10 +179,10 @@ def tile_multiheadselfattention_pa_t_kernel(tc, x, W, out_0, out_1, out_2):
                 scales=x_scales[:, 0 : n * P],
                 in_=grouped[:, 0 : n * P * PACK],
             )
-            return x_codes, x_scales
+            quantised[r] = (x_codes, x_scales)
 
-        def multiply_pair(k, quantised):
-            x_codes, x_scales = quantised
+        def multiply_pair(r, k):
+            x_codes, x_scales = quantised[r]
             qk_ps = psum_qk.tile([P, PAIR, ROTATED], F32, name="qk_ps")
             v_ps = psum_v.tile([P, PAIR, VALUES], F32, name="v_ps")
             for j in range(PAIR):
@@ -203,7 +209,7 @@ def tile_multiheadselfattention_pa_t_kernel(tc, x, W, out_0, out_1, out_2):
         qk_t = psum_v.tile([P, 2, 2, P], F32, name="v_ps")
         for chunk in range(2):
             transpose_words(nc, qk_t[:, chunk], w_rows[:, chunk, :], identity)
-        nc.vector.tensor_copy(out=w_words[:, 1:3], in_=qk_t[:].rearrange("p c u r -> p c r u"))
+        nc.scalar.copy(out=w_words[:, 1:3], in_=qk_t[:].rearrange("p c u r -> p c r u"))
         transpose_pair(0, 0)
         v_t = psum_v.tile([P, 2, 2, P], F32, name="v_ps")
         transpose_words(nc, v_t[:, 0], w_rows[:, 2, :], identity)
@@ -212,19 +218,21 @@ def tile_multiheadselfattention_pa_t_kernel(tc, x, W, out_0, out_1, out_2):
             scales=w_scales[:, VALUES:W_COLS],
             in_=w_grouped[:, VALUES * PACK : W_COLS * PACK],
         )
-        quantised = quantise_round(0)
-        nc.scalar.copy(out=w_words[:, 0], in_=v_t[:, 0].rearrange("p u r -> p r u"))
-        filled = MAX_ROUND
-        fill_rotation_table(nc, table, minus_abs, minus_frac, 0, filled)
-        for k in range(rounds[1][2] // PAIR):
-            transpose_pair(1, k)
+        quantised = {}
+        quantise_round(0)
+        nc.vector.tensor_copy(out=w_words[:, 0], in_=v_t[:, 0].rearrange("p u r -> p r u"))
         nc.vector.quantize_mx(
             out=w_codes[:, 0:VALUES].bitcast(FP8X4),
             scales=w_scales[:, 0:VALUES],
             in_=w_grouped[:, 0 : VALUES * PACK],
         )
+        filled = MAX_ROUND
+        fill_rotation_table(nc, table, minus_abs, minus_frac, 0, filled)
+        transpose_pair(1, 0)
+        transposed = 2
 
         store_index = 0
+        last_adds, last_stores = [], []
         for r, (b, first, n) in enumerate(rounds):
             store_first, store_n = stores[store_index][1:]
             slot = first - store_first
@@ -232,21 +240,21 @@ def tile_multiheadselfattention_pa_t_kernel(tc, x, W, out_0, out_1, out_2):
                 qk_out = results.tile([P, GROUPS, MAX_STORE, DH], F32, name="qk_out")
                 v_out = results.tile([P, H, MAX_STORE, DH], F32, name="v_out")
 
-            ahead_pairs = rounds[r + AHEAD][2] // PAIR if r + AHEAD < len(rounds) else 0
+            ahead = min(r + (AHEAD if r < len(rounds) // 2 else AHEAD + 1), len(rounds) - 1)
+            ahead_pairs = [(s, k) for s in range(transposed, ahead + 1) for k in range(rounds[s][2] // PAIR)]
+            transposed = max(transposed, ahead + 1)
             qk_banks = []
-            for k in range(max(ahead_pairs, n // PAIR)):
-                if k < ahead_pairs:
-                    transpose_pair(r + AHEAD, k)
+            for k in range(max(len(ahead_pairs), n // PAIR)):
+                if k < len(ahead_pairs):
+                    transpose_pair(*ahead_pairs[k])
                 if k < n // PAIR:
-                    qk_ps, v_ps = multiply_pair(k, quantised)
+                    qk_ps, v_ps = multiply_pair(r, k)
                     qk_banks.append(qk_ps)
                     lo = slot + PAIR * k
                     nc.scalar.copy(
                         out=v_out[:, :, lo : lo + PAIR, :].rearrange("p h j d -> p j h d"),
                         in_=v_ps[:].rearrange("p j (h d) -> p j h d", h=H),
                     )
-            if r + 1 < len(rounds):
-                quantised = quantise_round(r + 1)
             if filled < TILES:
                 fill_rotation_table(nc, table, minus_abs, minus_frac, filled, filled + MAX_ROUND)
                 filled += MAX_ROUND
@@ -255,28 +263,46 @@ def tile_multiheadselfattention_pa_t_kernel(tc, x, W, out_0, out_1, out_2):
             pair_shape = [P, PAIR, GROUPS, PAIRS, 2]
             for k in range(n // PAIR):
                 t = first + PAIR * k
-                qk = qk_banks[k][:].rearrange("p j (g i h) -> p j g i h", g=GROUPS, h=2)
-                for term, operand in ((0, qk), (1, qk[:, :, :, :, ::-1])):
+                for term in range(2):
                     nc.vector.tensor_tensor(
                         out=products[:, term, PAIR * k : PAIR * k + PAIR, :].rearrange(
                             "p j (g i h) -> p j g i h", g=GROUPS, h=2
                         ),
-                        in0=operand,
+                        in0=qk_banks[k][:].rearrange("p j (g i h) -> p j g i h", g=GROUPS, h=2),
                         in1=table[:, t : t + PAIR, term].unsqueeze(2).to_broadcast(pair_shape),
                         op=ALU.mult,
                     )
-            adder = nc.vector if r + 1 == len(rounds) else nc.gpsimd
-            adder.tensor_tensor(
-                out=qk_out[:, :, slot : slot + n, :].rearrange("p g j d -> p j g d"),
-                in0=products[:, 0, 0:n, :].rearrange("p j (g d) -> p j g d", g=GROUPS),
-                in1=products[:, 1, 0:n, :].rearrange("p j (g d) -> p j g d", g=GROUPS),
-                op=ALU.add,
-            )
+                    if r == 0 and term == 0:
+                        quantise_round(1)
+            while len(quantised) <= ahead:
+                quantise_round(len(quantised))
+            def add_terms(engine, products=products, qk_out=qk_out, slot=slot, n=n):
+                terms = products[:, :, 0:n, :].rearrange("p w j (g i h) -> p w j g i h", g=GROUPS, h=2)
+                engine.tensor_tensor(
+                    out=qk_out[:, :, slot : slot + n, :].rearrange("p g j (i h) -> p j g i h", h=2),
+                    in0=terms[:, 0],
+                    in1=terms[:, 1, :, :, :, ::-1],
+                    op=ALU.add,
+                )
+
+            def store(b=b, first=store_first, n=store_n, qk_out=qk_out):
+                for out, result in ((out_0, qk_out[:, 0:H]), (out_1, qk_out[:, H:GROUPS])):
+                    rows = out[b].rearrange("h (p t) d -> p h t d", t=TILES)
+                    nc.sync.dma_start(out=rows[:, :, first : first + n, :], in_=result[:, :, 0:n, :])
 
             if slot + n == store_n:
-                for out, result in ((out_2, v_out[:]), (out_0, qk_out[:, 0:H]), (out_1, qk_out[:, H:GROUPS])):
-                    rows = out[b].rearrange("h (p t) d -> p h t d", t=TILES)
-                    nc.sync.dma_start(
-                        out=rows[:, :, store_first : store_first + store_n, :], in_=result[:, :, 0:store_n, :]
-                    )
+                rows = out_2[b].rearrange("h (p t) d -> p h t d", t=TILES)
+                nc.sync.dma_start(
+                    out=rows[:, :, store_first : store_first + store_n, :], in_=v_out[:, :, 0:store_n, :]
+                )
                 store_index += 1
+            if r + 2 < len(rounds):
+                add_terms(nc.gpsimd)
+                if slot + n == store_n:
+                    store()
+            else:
+                last_adds.append(add_terms)
+                last_stores.append(store)
+        for add_terms, store in zip(last_adds, last_stores):
+            add_terms(nc.vector)
+            store()

@@ -21,7 +21,12 @@ PAIRS = DH // 2
 GROUPS = 2 * H
 ROTATED = GROUPS * DH
 VALUES = H * DH
-W_COLS = VALUES + ROTATED
+SUMS = ROTATED // 2
+V_COLS = slice(0, VALUES)
+QK_COLS = slice(VALUES, VALUES + ROTATED)
+FIRST_COLS = slice(QK_COLS.stop, QK_COLS.stop + SUMS)
+SECOND_COLS = slice(FIRST_COLS.stop, FIRST_COLS.stop + SUMS)
+W_COLS = SECOND_COLS.stop
 TILES = L // P
 PAIR = 2
 MAX_ROUND = 4
@@ -85,17 +90,16 @@ def rotation_turns(nc, consts, position):
     return minus_abs, minus_frac
 
 
-def fill_rotation_table(nc, table, minus_abs, minus_frac, lo, hi):
+def fill_tables(nc, sines, cos_table, cross_table, minus_abs, minus_frac, lo, hi):
     nc.scalar.activation(
-        out=table[:, lo:hi, 0],
-        in_=minus_abs[:, lo:hi].unsqueeze(3).to_broadcast([P, hi - lo, PAIRS, 2]),
-        func=ACT.Sin,
-        scale=2.0 * math.pi,
-        bias=0.5 * math.pi,
+        out=cos_table[:, lo:hi], in_=minus_abs[:, lo:hi], func=ACT.Sin, scale=2.0 * math.pi, bias=0.5 * math.pi
     )
     for h, sign in ((0, -1.0), (1, 1.0)):
         nc.scalar.activation(
-            out=table[:, lo:hi, 1, :, h], in_=minus_frac[:, lo:hi], func=ACT.Sin, scale=sign * 2.0 * math.pi
+            out=sines[:, h, lo:hi], in_=minus_frac[:, lo:hi], func=ACT.Sin, scale=sign * 2.0 * math.pi
+        )
+        nc.gpsimd.tensor_tensor(
+            out=cross_table[:, lo:hi, :, h], in0=sines[:, h, lo:hi], in1=cos_table[:, lo:hi], op=ALU.subtract
         )
 
 
@@ -114,8 +118,9 @@ def tile_multiheadselfattention_pa_t_kernel(tc, x, W, out_0, out_1, out_2):
         products_pool = ctx.enter_context(tc.tile_pool(name="products_pool", bufs=3))
         results = ctx.enter_context(tc.tile_pool(name="results", bufs=4))
         psum_xt = ctx.enter_context(tc.psum_pool(name="psum_xt", bufs=2))
-        psum_qk = ctx.enter_context(tc.psum_pool(name="psum_qk", bufs=4))
-        psum_v = ctx.enter_context(tc.psum_pool(name="psum_v", bufs=2))
+        psum_qk = ctx.enter_context(tc.psum_pool(name="psum_qk", bufs=3))
+        psum_sum = ctx.enter_context(tc.psum_pool(name="psum_sum", bufs=2))
+        psum_v = ctx.enter_context(tc.psum_pool(name="psum_v", bufs=1))
         ctx.enter_context(tc.manual_schedule())
 
         w_rows = consts.tile([P, 3, D], BF16)
@@ -151,7 +156,9 @@ def tile_multiheadselfattention_pa_t_kernel(tc, x, W, out_0, out_1, out_2):
         identity = consts.tile([P, P], F32)
         make_identity(nc, identity[:])
 
-        table = consts.tile([P, TILES, 2, PAIRS, 2], F32)
+        sines = consts.tile([P, 2, TILES, PAIRS], F32)
+        cos_table = consts.tile([P, TILES, PAIRS], F32)
+        cross_table = consts.tile([P, TILES, PAIRS, 2], F32)
         minus_abs, minus_frac = rotation_turns(nc, consts, position)
 
         grouped_rounds = {}
@@ -181,58 +188,81 @@ def tile_multiheadselfattention_pa_t_kernel(tc, x, W, out_0, out_1, out_2):
             )
             quantised[r] = (x_codes, x_scales)
 
-        def multiply_pair(r, k):
+        def multiply(r, j, cols, out, start=True, stop=True):
             x_codes, x_scales = quantised[r]
-            qk_ps = psum_qk.tile([P, PAIR, ROTATED], F32, name="qk_ps")
-            v_ps = psum_v.tile([P, PAIR, VALUES], F32, name="v_ps")
-            for j in range(PAIR):
-                tokens = slice((PAIR * k + j) * P, (PAIR * k + j + 1) * P)
-                for cols, acc in (
-                    (slice(VALUES, W_COLS), qk_ps[:, j, :]),
-                    (slice(0, VALUES), v_ps[:, j, :]),
-                ):
-                    nc.tensor.matmul_mx(
-                        out=acc,
-                        lhsT=x_codes[:, tokens].bitcast(FP8X4),
-                        lhsT_scale=x_scales[:, tokens],
-                        rhs=w_codes[:, cols].bitcast(FP8X4),
-                        rhs_scale=w_scales[:, cols],
-                        start=True,
-                        stop=True,
-                    )
-            return qk_ps, v_ps
+            tokens = slice(j * P, (j + 1) * P)
+            nc.tensor.matmul_mx(
+                out=out,
+                lhsT=x_codes[:, tokens].bitcast(FP8X4),
+                lhsT_scale=x_scales[:, tokens],
+                rhs=w_codes[:, cols].bitcast(FP8X4),
+                rhs_scale=w_scales[:, cols],
+                start=start,
+                stop=stop,
+            )
+
+        def multiply_round(r):
+            n = rounds[r][2]
+            qk_banks = []
+            for k in range(n // PAIR):
+                qk_ps = psum_qk.tile([P, PAIR, ROTATED], F32, name="qk_ps")
+                for j in range(PAIR):
+                    multiply(r, PAIR * k + j, QK_COLS, qk_ps[:, j, :])
+                qk_banks.append(qk_ps)
+                if k == 0:
+                    sum_ps = psum_sum.tile([P, MAX_ROUND, SUMS], F32, name="sum_ps")
+                    for j in range(n):
+                        multiply(r, j, FIRST_COLS, sum_ps[:, j, :], stop=False)
+                        multiply(r, j, SECOND_COLS, sum_ps[:, j, :], start=False)
+            v_ps = psum_v.tile([P, MAX_ROUND, VALUES], F32, name="v_ps")
+            for j in range(n):
+                multiply(r, j, V_COLS, v_ps[:, j, :])
+            return qk_banks, sum_ps, v_ps
 
         w_codes = consts.tile([P, W_COLS], U32, align_bytes=64)
         w_scales = consts.tile([P, W_COLS], U8, align_bytes=64)
         w_grouped = consts.tile([P, W_COLS * PACK], BF16, align_bytes=64)
-        w_words = w_grouped[:].bitcast(F32).rearrange("p (c r u) -> p c r u", c=3, u=2)
-        qk_t = psum_v.tile([P, 2, 2, P], F32, name="v_ps")
+        w_words = w_grouped[:].bitcast(F32).rearrange("p (c u) -> p c u", u=2)
+
+        def quantise_weights(cols):
+            nc.vector.quantize_mx(
+                out=w_codes[:, cols].bitcast(FP8X4),
+                scales=w_scales[:, cols],
+                in_=w_grouped[:, cols.start * PACK : cols.stop * PACK],
+            )
+
+        quantised = {}
+        qk_t = psum_sum.tile([P, 2, 2, P], F32, name="sum_ps")
         for chunk in range(2):
             transpose_words(nc, qk_t[:, chunk], w_rows[:, chunk, :], identity)
-        nc.scalar.copy(out=w_words[:, 1:3], in_=qk_t[:].rearrange("p c u r -> p c r u"))
+        nc.scalar.copy(
+            out=w_words[:, QK_COLS, :].rearrange("p (c r) u -> p c r u", c=2), in_=qk_t[:].rearrange("p c u r -> p c r u")
+        )
         transpose_pair(0, 0)
-        v_t = psum_v.tile([P, 2, 2, P], F32, name="v_ps")
+        v_t = psum_sum.tile([P, 2, 2, P], F32, name="sum_ps")
         transpose_words(nc, v_t[:, 0], w_rows[:, 2, :], identity)
-        nc.vector.quantize_mx(
-            out=w_codes[:, VALUES:W_COLS].bitcast(FP8X4),
-            scales=w_scales[:, VALUES:W_COLS],
-            in_=w_grouped[:, VALUES * PACK : W_COLS * PACK],
-        )
-        quantised = {}
+        for h, cols in enumerate((FIRST_COLS, SECOND_COLS)):
+            nc.vector.tensor_copy(
+                out=w_words[:, cols, :].rearrange("p (c m) u -> p c m u", c=2),
+                in_=qk_t[:].rearrange("p c u (m h) -> p h c m u", h=2)[:, h],
+            )
+        quantise_weights(QK_COLS)
         quantise_round(0)
-        nc.vector.tensor_copy(out=w_words[:, 0], in_=v_t[:, 0].rearrange("p u r -> p r u"))
-        nc.vector.quantize_mx(
-            out=w_codes[:, 0:VALUES].bitcast(FP8X4),
-            scales=w_scales[:, 0:VALUES],
-            in_=w_grouped[:, 0 : VALUES * PACK],
-        )
+        quantise_weights(slice(FIRST_COLS.start, SECOND_COLS.stop))
+        nc.vector.tensor_copy(out=w_words[:, V_COLS, :], in_=v_t[:, 0].rearrange("p u r -> p r u"))
+        quantise_weights(V_COLS)
         filled = MAX_ROUND
-        fill_rotation_table(nc, table, minus_abs, minus_frac, 0, filled)
+        fill_tables(nc, sines, cos_table, cross_table, minus_abs, minus_frac, 0, filled)
         transpose_pair(1, 0)
         transposed = 2
 
+        def store(out, b, first, n, result):
+            rows = out[b].rearrange("h (p t) d -> p h t d", t=TILES)
+            nc.sync.dma_start(out=rows[:, :, first : first + n, :], in_=result[:, :, 0:n, :])
+
         store_index = 0
-        last_adds, last_stores = [], []
+        last_rounds = []
+        gate = consts.tile([P, 4], U8)
         for r, (b, first, n) in enumerate(rounds):
             store_first, store_n = stores[store_index][1:]
             slot = first - store_first
@@ -241,68 +271,76 @@ def tile_multiheadselfattention_pa_t_kernel(tc, x, W, out_0, out_1, out_2):
                 v_out = results.tile([P, H, MAX_STORE, DH], F32, name="v_out")
 
             ahead = min(r + (AHEAD if r < len(rounds) // 2 else AHEAD + 1), len(rounds) - 1)
-            ahead_pairs = [(s, k) for s in range(transposed, ahead + 1) for k in range(rounds[s][2] // PAIR)]
+            for s in range(transposed, ahead + 1):
+                for k in range(rounds[s][2] // PAIR):
+                    transpose_pair(s, k)
             transposed = max(transposed, ahead + 1)
-            qk_banks = []
-            for k in range(max(len(ahead_pairs), n // PAIR)):
-                if k < len(ahead_pairs):
-                    transpose_pair(*ahead_pairs[k])
-                if k < n // PAIR:
-                    qk_ps, v_ps = multiply_pair(r, k)
-                    qk_banks.append(qk_ps)
-                    lo = slot + PAIR * k
-                    nc.scalar.copy(
-                        out=v_out[:, :, lo : lo + PAIR, :].rearrange("p h j d -> p j h d"),
-                        in_=v_ps[:].rearrange("p j (h d) -> p j h d", h=H),
-                    )
+            qk_banks, sum_ps, v_ps = multiply_round(r)
+            nc.scalar.copy(
+                out=v_out[:, :, slot : slot + n, :].rearrange("p h j d -> p j h d"),
+                in_=v_ps[:, 0:n, :].rearrange("p j (h d) -> p j h d", h=H),
+            )
             if filled < TILES:
-                fill_rotation_table(nc, table, minus_abs, minus_frac, filled, filled + MAX_ROUND)
+                fill_tables(nc, sines, cos_table, cross_table, minus_abs, minus_frac, filled, filled + MAX_ROUND)
                 filled += MAX_ROUND
 
-            products = products_pool.tile([P, 2, MAX_ROUND, ROTATED], F32, name="products")
-            pair_shape = [P, PAIR, GROUPS, PAIRS, 2]
-            for k in range(n // PAIR):
+            crossed = products_pool.tile([P, MAX_ROUND, ROTATED], F32, name="crossed")
+            summed = products_pool.tile([P, MAX_ROUND, SUMS], F32, name="summed")
+
+            def cross(k, r=r, first=first, qk_banks=qk_banks, crossed=crossed):
                 t = first + PAIR * k
-                for term in range(2):
-                    nc.vector.tensor_tensor(
-                        out=products[:, term, PAIR * k : PAIR * k + PAIR, :].rearrange(
-                            "p j (g i h) -> p j g i h", g=GROUPS, h=2
-                        ),
-                        in0=qk_banks[k][:].rearrange("p j (g i h) -> p j g i h", g=GROUPS, h=2),
-                        in1=table[:, t : t + PAIR, term].unsqueeze(2).to_broadcast(pair_shape),
-                        op=ALU.mult,
-                    )
-                    if r == 0 and term == 0:
-                        quantise_round(1)
-            while len(quantised) <= ahead:
-                quantise_round(len(quantised))
-            def add_terms(engine, products=products, qk_out=qk_out, slot=slot, n=n):
-                terms = products[:, :, 0:n, :].rearrange("p w j (g i h) -> p w j g i h", g=GROUPS, h=2)
+                nc.vector.tensor_tensor(
+                    out=crossed[:, PAIR * k : PAIR * k + PAIR, :].rearrange("p j (g d) -> p j g d", g=GROUPS),
+                    in0=qk_banks[k][:].rearrange("p j (g d) -> p j g d", g=GROUPS),
+                    in1=cross_table[:, t : t + PAIR]
+                    .rearrange("p j i h -> p j (i h)")
+                    .unsqueeze(2)
+                    .to_broadcast([P, PAIR, GROUPS, DH]),
+                    op=ALU.mult,
+                )
+
+            cross(0)
+            if r == 0:
+                quantise_round(1)
+            nc.vector.tensor_tensor(
+                out=summed[:, 0:n, :].rearrange("p j (g i) -> p j g i", g=GROUPS),
+                in0=sum_ps[:, 0:n, :].rearrange("p j (g i) -> p j g i", g=GROUPS),
+                in1=cos_table[:, first : first + n].unsqueeze(2).to_broadcast([P, n, GROUPS, PAIRS]),
+                op=ALU.mult,
+            )
+            if n > PAIR:
+                cross(1)
+
+            def add(engine, lo, hi, crossed=crossed, summed=summed, qk_out=qk_out, slot=slot):
                 engine.tensor_tensor(
-                    out=qk_out[:, :, slot : slot + n, :].rearrange("p g j (i h) -> p j g i h", h=2),
-                    in0=terms[:, 0],
-                    in1=terms[:, 1, :, :, :, ::-1],
+                    out=qk_out[:, :, slot + lo : slot + hi, :].rearrange("p g j (i h) -> p j g i h", h=2),
+                    in0=summed[:, lo:hi, :]
+                    .rearrange("p j (g i) -> p j g i", g=GROUPS)
+                    .unsqueeze(4)
+                    .to_broadcast([P, hi - lo, GROUPS, PAIRS, 2]),
+                    in1=crossed[:, lo:hi, :].rearrange("p j (g i h) -> p j g i h", g=GROUPS, h=2)[:, :, :, :, ::-1],
                     op=ALU.add,
                 )
 
-            def store(b=b, first=store_first, n=store_n, qk_out=qk_out):
-                for out, result in ((out_0, qk_out[:, 0:H]), (out_1, qk_out[:, H:GROUPS])):
-                    rows = out[b].rearrange("h (p t) d -> p h t d", t=TILES)
-                    nc.sync.dma_start(out=rows[:, :, first : first + n, :], in_=result[:, :, 0:n, :])
-
-            if slot + n == store_n:
-                rows = out_2[b].rearrange("h (p t) d -> p h t d", t=TILES)
-                nc.sync.dma_start(
-                    out=rows[:, :, store_first : store_first + store_n, :], in_=v_out[:, :, 0:store_n, :]
-                )
+            stored = slot + n == store_n
+            if stored:
+                store(out_2, b, store_first, store_n, v_out)
                 store_index += 1
-            if r + 2 < len(rounds):
-                add_terms(nc.gpsimd)
-                if slot + n == store_n:
-                    store()
-            else:
-                last_adds.append(add_terms)
-                last_stores.append(store)
-        for add_terms, store in zip(last_adds, last_stores):
-            add_terms(nc.vector)
-            store()
+            if r + 2 >= len(rounds):
+                last_rounds.append((add, n, b, store_first, store_n, qk_out))
+                continue
+            if n > PAIR:
+                add(nc.vector, 0, PAIR)
+            newest = len(quantised)
+            while len(quantised) <= ahead:
+                quantise_round(len(quantised))
+            if len(quantised) > newest:
+                nc.gpsimd.tensor_copy(out=gate[:], in_=quantised[len(quantised) - 1][1][:, 0:4])
+            add(nc.gpsimd, PAIR if n > PAIR else 0, n)
+            if stored:
+                store(out_0, b, store_first, store_n, qk_out[:, 0:H])
+                store(out_1, b, store_first, store_n, qk_out[:, H:GROUPS])
+        for add, n, b, store_first, store_n, qk_out in last_rounds:
+            add(nc.vector, 0, n)
+            store(out_0, b, store_first, store_n, qk_out[:, 0:H])
+            store(out_1, b, store_first, store_n, qk_out[:, H:GROUPS])

@@ -94,7 +94,7 @@ def fill_tables(nc, sines, cos_table, cross_table, minus_abs, minus_frac, lo, hi
     nc.scalar.activation(
         out=cos_table[:, lo:hi], in_=minus_abs[:, lo:hi], func=ACT.Sin, scale=2.0 * math.pi, bias=0.5 * math.pi
     )
-    for h, sign in ((0, -1.0), (1, 1.0)):
+    for h, sign in ((0, 1.0), (1, -1.0)):
         nc.scalar.activation(
             out=sines[:, h, lo:hi], in_=minus_frac[:, lo:hi], func=ACT.Sin, scale=sign * 2.0 * math.pi
         )
@@ -235,9 +235,11 @@ def tile_multiheadselfattention_pa_t_kernel(tc, x, W, out_0, out_1, out_2):
         qk_t = psum_sum.tile([P, 2, 2, P], F32, name="sum_ps")
         for chunk in range(2):
             transpose_words(nc, qk_t[:, chunk], w_rows[:, chunk, :], identity)
-        nc.scalar.copy(
-            out=w_words[:, QK_COLS, :].rearrange("p (c r) u -> p c r u", c=2), in_=qk_t[:].rearrange("p c u r -> p c r u")
-        )
+        swapped = w_words[:, QK_COLS, :].rearrange("p (c m h) u -> p h c m u", c=2, h=2)
+        for h in range(2):
+            nc.scalar.copy(
+                out=swapped[:, h], in_=qk_t[:].rearrange("p c u (m h) -> p h c m u", h=2)[:, 1 - h]
+            )
         transpose_pair(0, 0)
         v_t = psum_sum.tile([P, 2, 2, P], F32, name="sum_ps")
         transpose_words(nc, v_t[:, 0], w_rows[:, 2, :], identity)
@@ -318,7 +320,7 @@ def tile_multiheadselfattention_pa_t_kernel(tc, x, W, out_0, out_1, out_2):
                     .rearrange("p j (g i) -> p j g i", g=GROUPS)
                     .unsqueeze(4)
                     .to_broadcast([P, hi - lo, GROUPS, PAIRS, 2]),
-                    in1=crossed[:, lo:hi, :].rearrange("p j (g i h) -> p j g i h", g=GROUPS, h=2)[:, :, :, :, ::-1],
+                    in1=crossed[:, lo:hi, :].rearrange("p j (g i h) -> p j g i h", g=GROUPS, h=2),
                     op=ALU.add,
                 )
 

@@ -31,6 +31,7 @@ TILES = L // P
 PAIR = 2
 MAX_ROUND = 4
 MAX_STORE = 8
+VECTOR_TILES = 1
 DIRECT = 8
 AHEAD = 2
 
@@ -90,17 +91,28 @@ def rotation_turns(nc, consts, position):
     return minus_abs, minus_frac
 
 
-def fill_tables(nc, sines, cos_table, cross_table, minus_abs, minus_frac, lo, hi):
+def sign_turns(engine, signed_turns, minus_frac, signs, lo, hi):
+    shape = [P, (hi - lo) * PAIRS, 2]
+    engine.tensor_tensor(
+        out=signed_turns[:, lo:hi].rearrange("p t i h -> p (t i) h"),
+        in0=minus_frac[:, lo:hi].rearrange("p t i -> p (t i)").unsqueeze(2).to_broadcast(shape),
+        in1=signs[:].unsqueeze(1).to_broadcast(shape),
+        op=ALU.mult,
+    )
+
+
+def fill_tables(nc, sines, cos_table, cross_table, minus_abs, signed_turns, lo, hi):
     nc.scalar.activation(
         out=cos_table[:, lo:hi], in_=minus_abs[:, lo:hi], func=ACT.Sin, scale=2.0 * math.pi, bias=0.5 * math.pi
     )
-    for h, sign in ((0, 1.0), (1, -1.0)):
-        nc.scalar.activation(
-            out=sines[:, h, lo:hi], in_=minus_frac[:, lo:hi], func=ACT.Sin, scale=sign * 2.0 * math.pi
-        )
-        nc.gpsimd.tensor_tensor(
-            out=cross_table[:, lo:hi, :, h], in0=sines[:, h, lo:hi], in1=cos_table[:, lo:hi], op=ALU.subtract
-        )
+    nc.scalar.activation(out=sines[:, lo:hi], in_=signed_turns[:, lo:hi], func=ACT.Sin, scale=2.0 * math.pi)
+    shape = [P, (hi - lo) * PAIRS, 2]
+    nc.gpsimd.tensor_tensor(
+        out=cross_table[:, lo:hi].rearrange("p t i h -> p (t i) h"),
+        in0=sines[:, lo:hi].rearrange("p t i h -> p (t i) h"),
+        in1=cos_table[:, lo:hi].rearrange("p t i -> p (t i)").unsqueeze(2).to_broadcast(shape),
+        op=ALU.subtract,
+    )
 
 
 def transpose_words(nc, out, rows, identity):
@@ -156,10 +168,16 @@ def tile_multiheadselfattention_pa_t_kernel(tc, x, W, out_0, out_1, out_2):
         identity = consts.tile([P, P], F32)
         make_identity(nc, identity[:])
 
-        sines = consts.tile([P, 2, TILES, PAIRS], F32)
+        signed_turns = consts.tile([P, TILES, PAIRS, 2], F32)
+        sines = consts.tile([P, TILES, PAIRS, 2], F32)
         cos_table = consts.tile([P, TILES, PAIRS], F32)
         cross_table = consts.tile([P, TILES, PAIRS, 2], F32)
+        signs = consts.tile([P, 2], F32)
+        nc.gpsimd.memset(signs[:, 0:1], 1.0)
+        nc.gpsimd.memset(signs[:, 1:2], -1.0)
         minus_abs, minus_frac = rotation_turns(nc, consts, position)
+        sign_turns(nc.vector, signed_turns, minus_frac, signs, 0, MAX_ROUND)
+        sign_turns(nc.gpsimd, signed_turns, minus_frac, signs, MAX_ROUND, TILES)
 
         grouped_rounds = {}
 
@@ -235,10 +253,10 @@ def tile_multiheadselfattention_pa_t_kernel(tc, x, W, out_0, out_1, out_2):
         qk_t = psum_sum.tile([P, 2, 2, P], F32, name="sum_ps")
         for chunk in range(2):
             transpose_words(nc, qk_t[:, chunk], w_rows[:, chunk, :], identity)
-        swapped = w_words[:, QK_COLS, :].rearrange("p (c m h) u -> p h c m u", c=2, h=2)
-        for h in range(2):
+        for c in range(2):
             nc.scalar.copy(
-                out=swapped[:, h], in_=qk_t[:].rearrange("p c u (m h) -> p h c m u", h=2)[:, 1 - h]
+                out=w_words[:, QK_COLS, :].rearrange("p (c m h) u -> p c m h u", c=2, h=2)[:, c],
+                in_=qk_t[:, c].rearrange("p u (m h) -> p m h u", h=2)[:, :, ::-1],
             )
         transpose_pair(0, 0)
         v_t = psum_sum.tile([P, 2, 2, P], F32, name="sum_ps")
@@ -254,7 +272,7 @@ def tile_multiheadselfattention_pa_t_kernel(tc, x, W, out_0, out_1, out_2):
         nc.vector.tensor_copy(out=w_words[:, V_COLS, :], in_=v_t[:, 0].rearrange("p u r -> p r u"))
         quantise_weights(V_COLS)
         filled = MAX_ROUND
-        fill_tables(nc, sines, cos_table, cross_table, minus_abs, minus_frac, 0, filled)
+        fill_tables(nc, sines, cos_table, cross_table, minus_abs, signed_turns, 0, filled)
         transpose_pair(1, 0)
         transposed = 2
 
@@ -272,7 +290,7 @@ def tile_multiheadselfattention_pa_t_kernel(tc, x, W, out_0, out_1, out_2):
                 qk_out = results.tile([P, GROUPS, MAX_STORE, DH], F32, name="qk_out")
                 v_out = results.tile([P, H, MAX_STORE, DH], F32, name="v_out")
 
-            ahead = min(r + (AHEAD if r < len(rounds) // 2 else AHEAD + 1), len(rounds) - 1)
+            ahead = min(r + AHEAD, len(rounds) - 1)
             for s in range(transposed, ahead + 1):
                 for k in range(rounds[s][2] // PAIR):
                     transpose_pair(s, k)
@@ -283,7 +301,7 @@ def tile_multiheadselfattention_pa_t_kernel(tc, x, W, out_0, out_1, out_2):
                 in_=v_ps[:, 0:n, :].rearrange("p j (h d) -> p j h d", h=H),
             )
             if filled < TILES:
-                fill_tables(nc, sines, cos_table, cross_table, minus_abs, minus_frac, filled, filled + MAX_ROUND)
+                fill_tables(nc, sines, cos_table, cross_table, minus_abs, signed_turns, filled, filled + MAX_ROUND)
                 filled += MAX_ROUND
 
             crossed = products_pool.tile([P, MAX_ROUND, ROTATED], F32, name="crossed")
@@ -332,13 +350,13 @@ def tile_multiheadselfattention_pa_t_kernel(tc, x, W, out_0, out_1, out_2):
                 last_rounds.append((add, n, b, store_first, store_n, qk_out))
                 continue
             if n > PAIR:
-                add(nc.vector, 0, PAIR)
+                add(nc.vector, 0, VECTOR_TILES)
             newest = len(quantised)
             while len(quantised) <= ahead:
                 quantise_round(len(quantised))
             if len(quantised) > newest:
                 nc.gpsimd.tensor_copy(out=gate[:], in_=quantised[len(quantised) - 1][1][:, 0:4])
-            add(nc.gpsimd, PAIR if n > PAIR else 0, n)
+            add(nc.gpsimd, VECTOR_TILES if n > PAIR else 0, n)
             if stored:
                 store(out_0, b, store_first, store_n, qk_out[:, 0:H])
                 store(out_1, b, store_first, store_n, qk_out[:, H:GROUPS])

@@ -31,7 +31,7 @@ TILES = L // P
 PAIR = 2
 MAX_ROUND = 4
 MAX_STORE = 8
-VECTOR_TILES = 1
+VECTOR_TILES = 2
 DIRECT = 8
 AHEAD = 2
 
@@ -282,7 +282,6 @@ def tile_multiheadselfattention_pa_t_kernel(tc, x, W, out_0, out_1, out_2):
 
         store_index = 0
         last_rounds = []
-        gate = consts.tile([P, 4], U8)
         for r, (b, first, n) in enumerate(rounds):
             store_first, store_n = stores[store_index][1:]
             slot = first - store_first
@@ -351,12 +350,11 @@ def tile_multiheadselfattention_pa_t_kernel(tc, x, W, out_0, out_1, out_2):
                 continue
             if n > PAIR:
                 add(nc.vector, 0, VECTOR_TILES)
-            newest = len(quantised)
             while len(quantised) <= ahead:
                 quantise_round(len(quantised))
-            if len(quantised) > newest:
-                nc.gpsimd.tensor_copy(out=gate[:], in_=quantised[len(quantised) - 1][1][:, 0:4])
-            add(nc.gpsimd, VECTOR_TILES if n > PAIR else 0, n)
+            lo = VECTOR_TILES if n > PAIR else 0
+            nc.vector.memset(qk_out[:, 0, slot + lo, 0:1], 0.0)
+            add(nc.gpsimd, lo, n)
             if stored:
                 store(out_0, b, store_first, store_n, qk_out[:, 0:H])
                 store(out_1, b, store_first, store_n, qk_out[:, H:GROUPS])

@@ -295,10 +295,6 @@ def tile_multiheadselfattention_pa_t_kernel(tc, x, W, out_0, out_1, out_2):
                     transpose_pair(s, k)
             transposed = max(transposed, ahead + 1)
             qk_banks, sum_ps, v_ps = multiply_round(r)
-            nc.scalar.copy(
-                out=v_out[:, :, slot : slot + n, :].rearrange("p h j d -> p j h d"),
-                in_=v_ps[:, 0:n, :].rearrange("p j (h d) -> p j h d", h=H),
-            )
             if filled < TILES:
                 fill_tables(nc, sines, cos_table, cross_table, minus_abs, signed_turns, filled, filled + MAX_ROUND)
                 filled += MAX_ROUND
@@ -328,6 +324,19 @@ def tile_multiheadselfattention_pa_t_kernel(tc, x, W, out_0, out_1, out_2):
                 op=ALU.mult,
             )
             if n > PAIR:
+                doubled = products_pool.tile([P, VECTOR_TILES, ROTATED], F32, name="doubled")
+                nc.scalar.copy(
+                    out=doubled[:].rearrange("p j (m h) -> p (j m) h", h=2),
+                    in_=summed[:, 0:VECTOR_TILES, :]
+                    .rearrange("p j m -> p (j m)")
+                    .unsqueeze(2)
+                    .to_broadcast([P, VECTOR_TILES * SUMS, 2]),
+                )
+            nc.scalar.copy(
+                out=v_out[:, :, slot : slot + n, :].rearrange("p h j d -> p j h d"),
+                in_=v_ps[:, 0:n, :].rearrange("p j (h d) -> p j h d", h=H),
+            )
+            if n > PAIR:
                 cross(1)
 
             def add(engine, lo, hi, crossed=crossed, summed=summed, qk_out=qk_out, slot=slot):
@@ -348,10 +357,15 @@ def tile_multiheadselfattention_pa_t_kernel(tc, x, W, out_0, out_1, out_2):
             if r + 2 >= len(rounds):
                 last_rounds.append((add, n, b, store_first, store_n, qk_out))
                 continue
-            if n > PAIR:
-                add(nc.vector, 0, VECTOR_TILES)
             while len(quantised) <= ahead:
                 quantise_round(len(quantised))
+            if n > PAIR:
+                nc.vector.tensor_tensor(
+                    out=qk_out[:, :, slot : slot + VECTOR_TILES, :].rearrange("p g j d -> p j g d"),
+                    in0=doubled[:].rearrange("p j (g d) -> p j g d", g=GROUPS),
+                    in1=crossed[:, 0:VECTOR_TILES, :].rearrange("p j (g d) -> p j g d", g=GROUPS),
+                    op=ALU.add,
+                )
             lo = VECTOR_TILES if n > PAIR else 0
             nc.vector.memset(qk_out[:, 0, slot + lo, 0:1], 0.0)
             add(nc.gpsimd, lo, n)

import math
from contextlib import ExitStack

import concourse.mybir as mybir
from concourse.masks import make_identity

F32 = mybir.dt.float32
BF16 = mybir.dt.bfloat16
I32 = mybir.dt.int32
U32 = mybir.dt.uint32
U8 = mybir.dt.uint8
FP8X4 = mybir.dt.float8_e4m3fn_x4
ALU = mybir.AluOpType
ACT = mybir.ActivationFunctionType

B, L, D, H, DH = 4, 2048, 512, 2, 64
THETA = 100000.0
P = 128
PACK = 4
PAIRS = DH // 2
GROUPS = 2 * H
ROTATED = GROUPS * DH
VALUES = H * DH
SUMS = ROTATED // 2
V_COLS = slice(0, VALUES)
QK_COLS = slice(VALUES, VALUES + ROTATED)
FIRST_COLS = slice(QK_COLS.stop, QK_COLS.stop + SUMS)
SECOND_COLS = slice(FIRST_COLS.stop, FIRST_COLS.stop + SUMS)
W_COLS = SECOND_COLS.stop
TILES = L // P
PAIR = 2
MAX_ROUND = 4
MAX_STORE = 8
VECTOR_TILES = 2
DIRECT = 8
AHEAD = 2

FLOPS = 2 * B * L * D * 3 * H * DH


def plan():
    rounds, stores = [], []
    for b in range(B):
        sizes = [MAX_ROUND] * (TILES // MAX_ROUND)
        store_sizes = [MAX_STORE] * (TILES // MAX_STORE)
        if b == 0:
            sizes = [PAIR, PAIR] + sizes[1:]
        if b == B - 1:
            sizes = sizes[:-1] + [PAIR, PAIR]
            store_sizes = store_sizes[:-1] + [MAX_ROUND, PAIR, PAIR]
        for lengths, out in ((sizes, rounds), (store_sizes, stores)):
            first = 0
            for n in lengths:
                out.append((b, first, n))
                first += n
    return rounds, stores


def rotation_turns(nc, consts, position):
    turns = consts.tile([P, TILES, PAIRS], F32)
    for i in range(DIRECT):
        nc.vector.tensor_scalar(
            out=turns[:, :, i : i + 1],
            in0=position[:].unsqueeze(2),
            scalar1=THETA ** (-2.0 * i / DH) / (2.0 * math.pi),
            scalar2=None,
            op0=ALU.mult,
        )
    known = DIRECT
    while known < PAIRS:
        nc.vector.tensor_scalar(
            out=turns[:, :, known : 2 * known],
            in0=turns[:, :, 0:known],
            scalar1=THETA ** (-2.0 * known / DH),
            scalar2=None,
            op0=ALU.mult,
        )
        known *= 2
    whole = consts.tile([P, TILES, PAIRS], I32)
    nc.vector.tensor_copy(out=whole[:], in_=turns[:])
    frac = consts.tile([P, TILES, PAIRS], F32)
    nc.vector.tensor_tensor(out=frac[:], in0=turns[:], in1=whole[:], op=ALU.subtract)
    minus_frac = consts.tile([P, TILES, PAIRS], F32)
    nc.vector.scalar_tensor_tensor(
        out=minus_frac[:], in0=frac[:], scalar=0.5, in1=frac[:], op0=ALU.is_gt, op1=ALU.subtract
    )
    minus_abs = consts.tile([P, TILES, PAIRS], F32)
    nc.vector.scalar_tensor_tensor(
        out=minus_abs[:], in0=minus_frac[:], scalar=-1.0, in1=minus_frac[:], op0=ALU.mult, op1=ALU.min
    )
    return minus_abs, minus_frac


def sign_turns(engine, signed_turns, minus_frac, signs, lo, hi):
    shape = [P, (hi - lo) * PAIRS, 2]
    engine.tensor_tensor(
        out=signed_turns[:, lo:hi].rearrange("p t i h -> p (t i) h"),
        in0=minus_frac[:, lo:hi].rearrange("p t i -> p (t i)").unsqueeze(2).to_broadcast(shape),
        in1=signs[:].unsqueeze(1).to_broadcast(shape),
        op=ALU.mult,
    )


def fill_tables(nc, sines, cos_table, cross_table, minus_abs, signed_turns, lo, hi):
    nc.scalar.activation(
        out=cos_table[:, lo:hi], in_=minus_abs[:, lo:hi], func=ACT.Sin, scale=2.0 * math.pi, bias=0.5 * math.pi
    )
    nc.scalar.activation(out=sines[:, lo:hi], in_=signed_turns[:, lo:hi], func=ACT.Sin, scale=2.0 * math.pi)
    shape = [P, (hi - lo) * PAIRS, 2]
    nc.gpsimd.tensor_tensor(
        out=cross_table[:, lo:hi].rearrange("p t i h -> p (t i) h"),
        in0=sines[:, lo:hi].rearrange("p t i h -> p (t i) h"),
        in1=cos_table[:, lo:hi].rearrange("p t i -> p (t i)").unsqueeze(2).to_broadcast(shape),
        op=ALU.subtract,
    )


def transpose_words(nc, out, rows, identity):
    words = rows.bitcast(F32)
    for u in range(2):
        nc.tensor.transpose(out[:, u, :], words[:, u : 2 * P : 2], identity[:])


def tile_multiheadselfattention_pa_t_kernel(tc, x, W, out_0, out_1, out_2):
    nc = tc.nc
    rounds, stores = plan()
    with ExitStack() as ctx:
        consts = ctx.enter_context(tc.tile_pool(name="consts", bufs=1))
        stage = ctx.enter_context(tc.tile_pool(name="stage", bufs=5))
        products_pool = ctx.enter_context(tc.tile_pool(name="products_pool", bufs=3))
        results = ctx.enter_context(tc.tile_pool(name="results", bufs=4))
        psum_xt = ctx.enter_context(tc.psum_pool(name="psum_xt", bufs=2))
        psum_qk = ctx.enter_context(tc.psum_pool(name="psum_qk", bufs=3))
        psum_sum = ctx.enter_context(tc.psum_pool(name="psum_sum", bufs=2))
        psum_v = ctx.enter_context(tc.psum_pool(name="psum_v", bufs=1))
        ctx.enter_context(tc.manual_schedule())

        w_rows = consts.tile([P, 3, D], BF16)
        x_rows = []

        def load_weights(chunk):
            nc.sync.dma_start(out=w_rows[:, chunk, :], in_=W[chunk * P : (chunk + 1) * P, :])

        load_weights(0)
        load_weights(1)
        for r, (b, first, n) in enumerate(rounds):
            x_tile = consts.tile([P, n, D], BF16, name="x_tile%d" % r)
            nc.sync.dma_start(
                out=x_tile[:],
                in_=x[b].rearrange("(p t) c -> p t c", t=TILES)[:, first : first + n, :],
            )
            x_rows.append(x_tile)
            if r == 0:
                load_weights(2)

        warm = consts.tile([P, 2], F32)
        nc.vector.memset(warm[:], 0.0)
        nc.scalar.activation(out=warm[:, 1:2], in_=warm[:, 0:1], func=ACT.Sin)

        position = consts.tile([P, TILES], F32)
        nc.gpsimd.iota(
            position[:],
            pattern=[[1, TILES]],
            base=0,
            channel_multiplier=TILES,
            allow_small_or_imprecise_dtypes=True,
        )
        identity = consts.tile([P, P], F32)
        make_identity(nc, identity[:])

        signed_turns = consts.tile([P, TILES, PAIRS, 2], F32)
        sines = consts.tile([P, TILES, PAIRS, 2], F32)
        cos_table = consts.tile([P, TILES, PAIRS], F32)
        cross_table = consts.tile([P, TILES, PAIRS, 2], F32)
        signs = consts.tile([P, 2], F32)
        nc.gpsimd.memset(signs[:, 0:1], 1.0)
        nc.gpsimd.memset(signs[:, 1:2], -1.0)
        minus_abs, minus_frac = rotation_turns(nc, consts, position)
        sign_turns(nc.vector, signed_turns, minus_frac, signs, 0, MAX_ROUND)
        sign_turns(nc.gpsimd, signed_turns, minus_frac, signs, MAX_ROUND, TILES)

        grouped_rounds = {}

        def transpose_pair(r, k):
            if k == 0:
                grouped = stage.tile([P, MAX_ROUND * P * PACK], BF16, align_bytes=64, name="grouped")
                grouped_rounds[r] = grouped
            xt = psum_xt.tile([P, PAIR, 2, P], F32, name="xt")
            for j in range(PAIR):
                transpose_words(nc, xt[:, j], x_rows[r][:, PAIR * k + j, :], identity)
            grouped_words = grouped_rounds[r][:].bitcast(F32).rearrange("p (j r u) -> p j r u", j=MAX_ROUND, u=2)
            nc.scalar.copy(
                out=grouped_words[:, PAIR * k : PAIR * k + PAIR],
                in_=xt[:].rearrange("p j u r -> p j r u"),
            )

        def quantise_round(r):
            n = rounds[r][2]
            grouped = grouped_rounds.pop(r)
            x_codes = stage.tile([P, MAX_ROUND * P], U32, align_bytes=64, name="x_codes")
            x_scales = stage.tile([P, MAX_ROUND * P], U8, align_bytes=64, name="x_scales")
            nc.vector.quantize_mx(
                out=x_codes[:, 0 : n * P].bitcast(FP8X4),
                scales=x_scales[:, 0 : n * P],
                in_=grouped[:, 0 : n * P * PACK],
            )
            quantised[r] = (x_codes, x_scales)

        def multiply(r, j, cols, out, start=True, stop=True):
            x_codes, x_scales = quantised[r]
            tokens = slice(j * P, (j + 1) * P)
            nc.tensor.matmul_mx(
                out=out,
                lhsT=x_codes[:, tokens].bitcast(FP8X4),
                lhsT_scale=x_scales[:, tokens],
                rhs=w_codes[:, cols].bitcast(FP8X4),
                rhs_scale=w_scales[:, cols],
                start=start,
                stop=stop,
            )

        def multiply_round(r):
            n = rounds[r][2]
            qk_banks = []
            for k in range(n // PAIR):
                qk_ps = psum_qk.tile([P, PAIR, ROTATED], F32, name="qk_ps")
                for j in range(PAIR):
                    multiply(r, PAIR * k + j, QK_COLS, qk_ps[:, j, :])
                qk_banks.append(qk_ps)
                if k == 0:
                    sum_ps = psum_sum.tile([P, MAX_ROUND, SUMS], F32, name="sum_ps")
                    for j in range(n):
                        multiply(r, j, FIRST_COLS, sum_ps[:, j, :], stop=False)
                        multiply(r, j, SECOND_COLS, sum_ps[:, j, :], start=False)
            v_ps = psum_v.tile([P, MAX_ROUND, VALUES], F32, name="v_ps")
            for j in range(n):
                multiply(r, j, V_COLS, v_ps[:, j, :])
            return qk_banks, sum_ps, v_ps

        w_codes = consts.tile([P, W_COLS], U32, align_bytes=64)
        w_scales = consts.tile([P, W_COLS], U8, align_bytes=64)
        w_grouped = consts.tile([P, W_COLS * PACK], BF16, align_bytes=64)
        w_words = w_grouped[:].bitcast(F32).rearrange("p (c u) -> p c u", u=2)

        def quantise_weights(cols):
            nc.vector.quantize_mx(
                out=w_codes[:, cols].bitcast(FP8X4),
                scales=w_scales[:, cols],
                in_=w_grouped[:, cols.start * PACK : cols.stop * PACK],
            )

        quantised = {}
        qk_t = psum_sum.tile([P, 2, 2, P], F32, name="sum_ps")
        for chunk in range(2):
            transpose_words(nc, qk_t[:, chunk], w_rows[:, chunk, :], identity)
        for c in range(2):
            nc.scalar.copy(
                out=w_words[:, QK_COLS, :].rearrange("p (c m h) u -> p c m h u", c=2, h=2)[:, c],
                in_=qk_t[:, c].rearrange("p u (m h) -> p m h u", h=2)[:, :, ::-1],
            )
        transpose_pair(0, 0)
        v_t = psum_sum.tile([P, 2, 2, P], F32, name="sum_ps")
        transpose_words(nc, v_t[:, 0], w_rows[:, 2, :], identity)
        for h, cols in enumerate((FIRST_COLS, SECOND_COLS)):
            nc.vector.tensor_copy(
                out=w_words[:, cols, :].rearrange("p (c m) u -> p c m u", c=2),
                in_=qk_t[:].rearrange("p c u (m h) -> p h c m u", h=2)[:, h],
            )
        quantise_weights(QK_COLS)
        quantise_round(0)
        quantise_weights(slice(FIRST_COLS.start, SECOND_COLS.stop))
        nc.vector.tensor_copy(out=w_words[:, V_COLS, :], in_=v_t[:, 0].rearrange("p u r -> p r u"))
        quantise_weights(V_COLS)
        filled = MAX_ROUND
        fill_tables(nc, sines, cos_table, cross_table, minus_abs, signed_turns, 0, filled)
        transpose_pair(1, 0)
        transposed = 2

        def store(out, b, first, n, result):
            rows = out[b].rearrange("h (p t) d -> p h t d", t=TILES)
            nc.sync.dma_start(out=rows[:, :, first : first + n, :], in_=result[:, :, 0:n, :])

        store_index = 0
        last_rounds = []
        for r, (b, first, n) in enumerate(rounds):
            store_first, store_n = stores[store_index][1:]
            slot = first - store_first
            if slot == 0:
                qk_out = results.tile([P, GROUPS, MAX_STORE, DH], F32, name="qk_out")
                v_out = results.tile([P, H, MAX_STORE, DH], F32, name="v_out")

            ahead = min(r + AHEAD, len(rounds) - 1)
            for s in range(transposed, ahead + 1):
                for k in range(rounds[s][2] // PAIR):
                    transpose_pair(s, k)
            transposed = max(transposed, ahead + 1)
            qk_banks, sum_ps, v_ps = multiply_round(r)
            if filled < TILES:
                fill_tables(nc, sines, cos_table, cross_table, minus_abs, signed_turns, filled, filled + MAX_ROUND)
                filled += MAX_ROUND

            crossed = products_pool.tile([P, MAX_ROUND, ROTATED], F32, name="crossed")
            summed = products_pool.tile([P, MAX_ROUND, SUMS], F32, name="summed")

            def cross(k, r=r, first=first, qk_banks=qk_banks, crossed=crossed):
                t = first + PAIR * k
                nc.vector.tensor_tensor(
                    out=crossed[:, PAIR * k : PAIR * k + PAIR, :].rearrange("p j (g d) -> p j g d", g=GROUPS),
                    in0=qk_banks[k][:].rearrange("p j (g d) -> p j g d", g=GROUPS),
                    in1=cross_table[:, t : t + PAIR]
                    .rearrange("p j i h -> p j (i h)")
                    .unsqueeze(2)
                    .to_broadcast([P, PAIR, GROUPS, DH]),
                    op=ALU.mult,
                )

            cross(0)
            if r == 0:
                quantise_round(1)
            nc.vector.tensor_tensor(
                out=summed[:, 0:n, :].rearrange("p j (g i) -> p j g i", g=GROUPS),
                in0=sum_ps[:, 0:n, :].rearrange("p j (g i) -> p j g i", g=GROUPS),
                in1=cos_table[:, first : first + n].unsqueeze(2).to_broadcast([P, n, GROUPS, PAIRS]),
                op=ALU.mult,
            )
            if n > PAIR:
                doubled = products_pool.tile([P, VECTOR_TILES, ROTATED], F32, name="doubled")
                nc.scalar.copy(
                    out=doubled[:].rearrange("p j (m h) -> p (j m) h", h=2),
                    in_=summed[:, 0:VECTOR_TILES, :]
                    .rearrange("p j m -> p (j m)")
                    .unsqueeze(2)
                    .to_broadcast([P, VECTOR_TILES * SUMS, 2]),
                )
            nc.scalar.copy(
                out=v_out[:, :, slot : slot + n, :].rearrange("p h j d -> p j h d"),
                in_=v_ps[:, 0:n, :].rearrange("p j (h d) -> p j h d", h=H),
            )
            if n > PAIR:
                cross(1)

            def add(engine, lo, hi, crossed=crossed, summed=summed, qk_out=qk_out, slot=slot):
                engine.tensor_tensor(
                    out=qk_out[:, :, slot + lo : slot + hi, :].rearrange("p g j (i h) -> p j g i h", h=2),
                    in0=summed[:, lo:hi, :]
                    .rearrange("p j (g i) -> p j g i", g=GROUPS)
                    .unsqueeze(4)
                    .to_broadcast([P, hi - lo, GROUPS, PAIRS, 2]),
                    in1=crossed[:, lo:hi, :].rearrange("p j (g i h) -> p j g i h", g=GROUPS, h=2),
                    op=ALU.add,
                )

            stored = slot + n == store_n
            if stored:
                store(out_2, b, store_first, store_n, v_out)
                store_index += 1
            if r + 2 >= len(rounds):
                last_rounds.append((add, n, b, store_first, store_n, qk_out))
                continue
            while len(quantised) <= ahead:
                quantise_round(len(quantised))
            if n > PAIR:
                nc.vector.tensor_tensor(
                    out=qk_out[:, :, slot : slot + VECTOR_TILES, :].rearrange("p g j d -> p j g d"),
                    in0=doubled[:].rearrange("p j (g d) -> p j g d", g=GROUPS),
                    in1=crossed[:, 0:VECTOR_TILES, :].rearrange("p j (g d) -> p j g d", g=GROUPS),
                    op=ALU.add,
                )
            lo = VECTOR_TILES if n > PAIR else 0
            nc.vector.memset(qk_out[:, 0, slot + lo, 0:1], 0.0)
            add(nc.gpsimd, lo, n)
            if stored:
                store(out_0, b, store_first, store_n, qk_out[:, 0:H])
                store(out_1, b, store_first, store_n, qk_out[:, H:GROUPS])
        for add, n, b, store_first, store_n, qk_out in last_rounds:
            add(nc.vector, 0, n)
            store(out_0, b, store_first, store_n, qk_out[:, 0:H])
            store(out_1, b, store_first, store_n, qk_out[:, H:GROUPS])
